import numpy as np
import ml_dtypes


def mxq(x, axis, fmt="e4m3"):
    dtype, down = {"e4m3": (ml_dtypes.float8_e4m3fn, 7), "e5m2": (ml_dtypes.float8_e5m2, 14)}[fmt]
    v = np.moveaxis(np.asarray(x, np.float32).astype(ml_dtypes.bfloat16).astype(np.float64), axis, -1)
    blocks = v.reshape(v.shape[:-1] + (-1, 32))
    amax = np.abs(blocks).max(-1, keepdims=True)
    byte = np.maximum(np.where(amax > 0, np.frexp(amax)[1] - 1 + 127, 0) - down, 1)
    scale = np.exp2(byte - 127.0)
    codes = (blocks / scale).astype(np.float32).astype(dtype).astype(np.float64)
    return np.moveaxis((codes * scale).reshape(v.shape), -1, axis)


BF16 = ml_dtypes.bfloat16


def bf(x):
    return np.asarray(x, np.float32).astype(BF16)


def f64(x):
    return np.asarray(x).astype(np.float64)


B, C, H, W, K, G = 2, 512, 32, 32, 1024, 8
N = B * H * W
EPS = 1e-12


def l2norm(v):
    n = np.sqrt((v * v).sum(-1, keepdims=True))
    return v / np.maximum(n, EPS)


def setup_inputs():
    cen = np.random.standard_normal((G, C))
    sgn = np.sign(np.random.standard_normal((K, 1)))
    gain = np.exp(0.5 * np.random.standard_normal((K, 1)))
    memory = 0.5 * gain * (2.0 * sgn * cen[np.random.randint(0, G, K)] + np.random.standard_normal((K, C)))
    amp = 3.0 * np.random.random((N, 1))
    feat = amp * cen[np.random.randint(0, G, N)] + np.random.standard_normal((N, C))
    x = np.ascontiguousarray(feat.reshape(B, H, W, C).transpose(0, 3, 1, 2))
    return {"x": bf(x), "memory": bf(memory)}


def reference(x, memory):
    feat = f64(x).transpose(0, 2, 3, 1).reshape(N, C)
    feat_norm = l2norm(feat)
    mem_norm = l2norm(f64(memory))
    sim = mxq(feat_norm, 1, "e4m3") @ mxq(mem_norm, 1, "e4m3").T
    e = np.exp(sim - sim.max(1, keepdims=True))
    z = e.sum(1, keepdims=True)
    recon = (mxq(e, 1, "e4m3") @ mxq(mem_norm, 0, "e4m3")) / z
    match_map = (e / z).max(1)
    return recon.reshape(B, H, W, C).transpose(0, 3, 1, 2), match_map.reshape(B, H, W)

@@ -1,0 +1,366 @@
+from contextlib import ExitStack
+
+import concourse.mybir as mybir
+from concourse.masks import make_identity
+
+F32 = mybir.dt.float32
+BF16 = mybir.dt.bfloat16
+U32 = mybir.dt.uint32
+U8 = mybir.dt.uint8
+FP8X4 = mybir.dt.float8_e4m3fn_x4
+ALU = mybir.AluOpType
+ACT = mybir.ActivationFunctionType
+AX = mybir.AxisListType
+
+P = 128
+B, C, HW, K = 2, 512, 1024, 1024
+N = B * HW
+NT = N // P
+FLOPS = 2 * N * K * C * 2
+
+
+def tile_memorybank2d_pa_kernel(tc, x, memory, out_0, out_1):
+    nc = tc.nc
+    with ExitStack() as ctx:
+        keep = ctx.enter_context(tc.tile_pool(name="keep", bufs=1))
+        small = ctx.enter_context(tc.tile_pool(name="small", bufs=6))
+        work = ctx.enter_context(tc.tile_pool(name="work", bufs=4))
+        ps_sim = ctx.enter_context(tc.psum_pool(name="ps_sim", bufs=4))
+        ps_tp = ctx.enter_context(tc.psum_pool(name="ps_tp", bufs=2))
+        ps_acc = ctx.enter_context(tc.psum_pool(name="ps_acc", bufs=1))
+        ps_bc = ctx.enter_context(tc.psum_pool(name="ps_bc", bufs=1))
+
+        mem_sb = keep.tile([P, 2, 4, C], BF16)
+        mem_v = memory.rearrange("(g p j) c -> g p j c", g=2, p=P, j=4)
+        x_sb = keep.tile([P, B, 4, HW], BF16)
+        x_v = x.rearrange("b (t p) h w -> b p t (h w)", p=P)
+        nc.sync.dma_start(out=mem_sb[:, 0], in_=mem_v[0])
+        nc.sync.dma_start(out=mem_sb[:, 1], in_=mem_v[1])
+        nc.sync.dma_start(out=x_sb[:, 0, :, 0:512], in_=x_v[0][:, :, 0:512])
+        nc.sync.dma_start(out=x_sb[:, 0, :, 512:1024], in_=x_v[0][:, :, 512:1024])
+        nc.sync.dma_start(out=x_sb[:, 1], in_=x_v[1])
+
+        ident_bf = keep.tile([P, P], BF16)
+        make_identity(nc, ident_bf[:])
+        ident_f = keep.tile([P, P], F32)
+        make_identity(nc, ident_f[:])
+        nhalf = keep.tile([P, 4], F32)
+        nc.vector.memset(nhalf[:], -0.5)
+        warm = keep.tile([P, 1], F32)
+        nc.vector.memset(warm[:], 0.0)
+        warm2 = keep.tile([P, 1], F32)
+        nc.scalar.activation(out=warm2[:], in_=warm[:], func=ACT.Exp)
+
+        def rsqrt_cols(dst, src, shape, expo):
+            cl = small.tile(shape, F32, name="cl")
+            nc.gpsimd.tensor_scalar(out=cl[:], in0=src, scalar1=3.0e38, scalar2=1.0e-24,
+                                    op0=ALU.min, op1=ALU.max)
+            nc.gpsimd.tensor_tensor(out=dst, in0=cl[:], in1=expo, op=ALU.pow)
+
+        rnx = {}
+        fc = keep.tile([P, N], U32, align_bytes=64)
+        fs = keep.tile([P, N], U8, align_bytes=64)
+        st = {}
+
+        def xgram(q, pool, tag):
+            b, n0 = q // 2, (q % 2) * 512
+            gram = pool.tile([P, 4, P], F32, tag=tag, name="gram")
+            for a in range(4):
+                cols = slice(n0 + a * P, n0 + (a + 1) * P)
+                for t in range(4):
+                    nc.tensor.matmul(gram[:, a, :], lhsT=x_sb[:, b, t, cols], rhs=x_sb[:, b, t, cols],
+                                     start=(t == 0), stop=(t == 3))
+            st[("gram", q)] = gram
+
+        def xdiag(q):
+            gram = st[("gram", q)]
+            ssx = small.tile([P, 4], F32, name="ssx")
+            for a in range(4):
+                junkd = work.tile([P, P], F32, name="junkd")
+                nc.vector.scalar_tensor_tensor(
+                    out=junkd[:], in0=gram[:, a, :], scalar=1.0, in1=ident_f[:],
+                    op0=ALU.mult, op1=ALU.mult, accum_out=ssx[:, a:a + 1])
+            st[("ssx", q)] = ssx
+
+        def xrsqrt(q):
+            rq = keep.tile([P, 4], F32, name="rnx%d" % q)
+            rsqrt_cols(rq[:], st[("ssx", q)][:], [P, 4], nhalf[:])
+            rnx[q] = rq
+
+        def xbcast(q, pool, tag):
+            rnb = pool.tile([P, 4, P], F32, tag=tag, name="rnb")
+            for a in range(4):
+                nc.tensor.matmul(rnb[:, a, :], lhsT=rnx[q][:, a:a + 1].to_broadcast([P, P]),
+                                 rhs=ident_f[:], start=True, stop=True)
+            st[("rnb", q)] = rnb
+
+        def xview(q, a):
+            b, n0 = q // 2, (q % 2) * 512 + a * P
+            return x_sb[:, b, :, n0:n0 + P].rearrange("p t n -> p n t")
+
+        def xquant(q, a0, na):
+            fg = st[("fg", q)]
+            lo, hi = q * 512 + a0 * P, q * 512 + (a0 + na) * P
+            nc.vector.quantize_mx(
+                out=fc[:, lo:hi].bitcast(FP8X4), scales=fs[:, lo:hi],
+                in_=fg[:, a0 * P:(a0 + na) * P, :].rearrange("p n t -> p (n t)"))
+
+        def xcopy(q):
+            rnbs = work.tile([P, 512], F32, name="rnbs", bufs=2)
+            nc.scalar.copy(out=rnbs[:], in_=st[("rnb", q)][:].rearrange("p a n -> p (a n)"))
+            st[("rnbs", q)] = rnbs
+            st[("fg", q)] = work.tile([P, 512, 4], BF16, name="fgl", bufs=2, align_bytes=64)
+
+        def xmul(q, a):
+            nc.gpsimd.tensor_tensor(
+                out=st[("fg", q)][:, a * P:(a + 1) * P, :], in0=xview(q, a),
+                in1=st[("rnbs", q)][:, a * P:(a + 1) * P].unsqueeze(2).to_broadcast([P, P, 4]),
+                op=ALU.mult)
+
+        ss_all = keep.tile([P, 2, 8], F32)
+        rn_all = keep.tile([P, 2, 8], F32)
+        mn_sb = keep.tile([P, 2, 4, C], BF16)
+        g1 = keep.tile([P, 8, P, 4], BF16, align_bytes=64)
+        m1c = keep.tile([P, K], U32, align_bytes=64)
+        m1s = keep.tile([P, K], U8, align_bytes=64)
+        g2 = keep.tile([P, 2, C, 4], BF16, align_bytes=64)
+        m2c = keep.tile([P, 2, C], U32, align_bytes=64)
+        m2s = keep.tile([P, 2, C], U8, align_bytes=64)
+
+        def mem_ss(g):
+            for jj in range(2):
+                junkv = work.tile([P, C], F32, name="junkv")
+                nc.vector.scalar_tensor_tensor(
+                    out=junkv[:], in0=mem_sb[:, g, jj, :], scalar=1.0, in1=mem_sb[:, g, jj, :],
+                    op0=ALU.mult, op1=ALU.mult, accum_out=ss_all[:, 0, 2 * g + jj:2 * g + jj + 1])
+                junks = work.tile([P, C], F32, name="junks")
+                nc.scalar.activation(out=junks[:], in_=mem_sb[:, g, 2 + jj, :], func=ACT.Square,
+                                     accum_out=ss_all[:, 1, 2 * g + jj:2 * g + jj + 1])
+
+        def mem_rsqrt(g):
+            rsqrt_cols(rn_all[:, :, 2 * g:2 * g + 2], ss_all[:, :, 2 * g:2 * g + 2], [P, 2, 2],
+                       nhalf[:].rearrange("p (a b) -> p a b", a=2))
+
+        def mem_scale(g):
+            for j in range(4):
+                rcol = rn_all[:, j // 2, 2 * g + j % 2:2 * g + j % 2 + 1]
+                if j < 3:
+                    nc.vector.tensor_scalar(out=mn_sb[:, g, j, :], in0=mem_sb[:, g, j, :],
+                                            scalar1=rcol, scalar2=None, op0=ALU.mult)
+                else:
+                    nc.scalar.activation(out=mn_sb[:, g, j, :], in_=mem_sb[:, g, j, :],
+                                         func=ACT.Copy, scale=rcol)
+
+        def mem_flip(g):
+            for jp in range(2):
+                tp = ps_tp.tile([P, 2, 4, P], BF16, tag="tp", name="tpm")
+                for jj in range(2):
+                    for t in range(4):
+                        nc.tensor.transpose(tp[:, jj, t, :], mn_sb[:, g, 2 * jp + jj, t * P:(t + 1) * P],
+                                            ident_bf[:])
+                st[("tpm", g, jp)] = tp
+
+        def mem_evac(g):
+            for jp in range(2):
+                r0 = 4 * g + 2 * jp
+                src = st[("tpm", g, jp)][:].rearrange("p r t k -> p r k t")
+                if jp == 0:
+                    nc.vector.tensor_copy(out=g1[:, r0:r0 + 2], in_=src)
+                else:
+                    nc.scalar.copy(out=g1[:, r0:r0 + 2], in_=src)
+
+        def mem_quant1(g):
+            nc.vector.quantize_mx(
+                out=m1c[:, g * 512:(g + 1) * 512].bitcast(FP8X4),
+                scales=m1s[:, g * 512:(g + 1) * 512],
+                in_=g1[:, 4 * g:4 * g + 4].rearrange("p r k t -> p (r k t)"))
+
+        def mem_group2(g):
+            nc.gpsimd.tensor_scalar(out=g2[:, g], in0=mn_sb[:, g].rearrange("p j c -> p c j"),
+                                    scalar1=1.0, scalar2=0.0, op0=ALU.mult, op1=ALU.add)
+
+        def mem_quant2(g):
+            nc.vector.quantize_mx(out=m2c[:, g, :].bitcast(FP8X4), scales=m2s[:, g, :],
+                                  in_=g2[:, g].rearrange("p c j -> p (c j)"))
+
+        def xmul0(a):
+            nc.vector.tensor_tensor(
+                out=st[("fg", 0)][:, a * P:(a + 1) * P, :], in0=xview(0, a),
+                in1=st[("rnb", 0)][:, a, :].unsqueeze(2).to_broadcast([P, P, 4]), op=ALU.mult)
+
+        rz_all = keep.tile([P, N], F32)
+        out_v = out_0.rearrange("b (cc p) h w -> b p cc (h w)", p=P)
+        out1_v = out_1.rearrange("b h w -> b (h w)")
+
+        def mm1(i):
+            sims = []
+            for h in range(2):
+                sim = ps_sim.tile([P, 512], F32, tag="sim", name="sim")
+                nc.tensor.matmul_mx(
+                    out=sim[:],
+                    lhsT=fc[:, i * P:(i + 1) * P].bitcast(FP8X4), lhsT_scale=fs[:, i * P:(i + 1) * P],
+                    rhs=m1c[:, h * 512:(h + 1) * 512].bitcast(FP8X4),
+                    rhs_scale=m1s[:, h * 512:(h + 1) * 512], start=True, stop=True)
+                sims.append(sim)
+            st[("sim", i)] = sims
+
+        def rowmax(i):
+            sims = st[("sim", i)]
+            nm2 = small.tile([P, 2], F32, name="nm2")
+            for h in range(2):
+                nc.vector.tensor_reduce(out=nm2[:, h:h + 1], in_=sims[h][:], axis=AX.X, op=ALU.max,
+                                        negate=True)
+            nmax = small.tile([P, 1], F32, name="nmax")
+            nc.vector.tensor_tensor(out=nmax[:], in0=nm2[:, 0:1], in1=nm2[:, 1:2], op=ALU.min)
+            st[("nmax", i)] = nmax
+
+        def expo(i):
+            sims = st[("sim", i)]
+            e = work.tile([P, K], BF16, name="e")
+            z2 = small.tile([P, 2], F32, name="z2")
+            for h in range(2):
+                nc.scalar.activation(out=e[:, h * 512:(h + 1) * 512], in_=sims[h][:], func=ACT.Exp,
+                                     bias=st[("nmax", i)][:], scale=1.0, accum_out=z2[:, h:h + 1])
+            st[("e", i)] = e
+            st[("z2", i)] = z2
+
+        def zchain(i):
+            z2 = st[("z2", i)]
+            zs = small.tile([P, 1], F32, name="zs")
+            nc.vector.tensor_tensor(out=zs[:], in0=z2[:, 0:1], in1=z2[:, 1:2], op=ALU.add)
+            rz = small.tile([P, 1], F32, name="rz")
+            nc.vector.reciprocal(out=rz[:], in_=zs[:])
+            st[("rz", i)] = rz
+
+        def flip(i):
+            e = st[("e", i)]
+            et = ps_tp.tile([P, 8, P], BF16, tag="tp", name="et")
+            for r in range(8):
+                nc.tensor.transpose(et[:, r, :], e[:, r * P:(r + 1) * P], ident_bf[:])
+            st[("et", i)] = et
+
+        def evac(i):
+            eg = work.tile([P, 2, P, 4], BF16, name="eg", align_bytes=64)
+            src = st[("et", i)][:].rearrange("p (g j) n -> p g n j", g=2)
+            if i % 4 == 3 and i > 3:
+                nc.vector.tensor_copy(out=eg[:], in_=src)
+            else:
+                nc.scalar.copy(out=eg[:], in_=src)
+            st[("eg", i)] = eg
+
+        def equant(i):
+            ec = work.tile([P, 2 * P], U32, name="ec", align_bytes=64)
+            es = work.tile([P, 2 * P], U8, name="es", align_bytes=64)
+            nc.vector.quantize_mx(out=ec[:].bitcast(FP8X4), scales=es[:],
+                                  in_=st[("eg", i)][:].rearrange("p g n j -> p (g n j)"))
+            st[("ec", i)] = (ec, es)
+
+        def zbcast(i):
+            zb = ps_bc.tile([P, P], F32, tag="bc", name="zb")
+            nc.tensor.matmul(zb[:], lhsT=st[("rz", i)][:, 0:1].to_broadcast([P, P]), rhs=ident_f[:],
+                             start=True, stop=True)
+            st[("zb", i)] = zb
+
+        def zcopy(i):
+            nc.scalar.copy(out=rz_all[:, i * P:(i + 1) * P], in_=st[("zb", i)][:])
+
+        def mm2(i):
+            ec, es = st[("ec", i)]
+            acc = ps_acc.tile([P, 4, P], F32, tag="acc", name="acc")
+            for cc in range(4):
+                for g in range(2):
+                    nc.tensor.matmul_mx(
+                        out=acc[:, cc, :],
+                        lhsT=m2c[:, g, cc * P:(cc + 1) * P].bitcast(FP8X4),
+                        lhsT_scale=m2s[:, g, cc * P:(cc + 1) * P],
+                        rhs=ec[:, g * P:(g + 1) * P].bitcast(FP8X4), rhs_scale=es[:, g * P:(g + 1) * P],
+                        start=(g == 0), stop=(g == 1))
+            st[("acc", i)] = acc
+
+        def finish(i):
+            if i % 2 == 0:
+                st["osb"] = work.tile([P, 4, 2 * P], F32, name="osb")
+            osb = st["osb"]
+            off = (i % 2) * P
+            nc.vector.tensor_tensor(
+                out=osb[:, :, off:off + P], in0=st[("acc", i)][:],
+                in1=rz_all[:, i * P:(i + 1) * P].unsqueeze(1).to_broadcast([P, 4, P]), op=ALU.mult)
+            if i % 2 == 1:
+                b, n0 = i // 8, ((i - 1) % 8) * P
+                nc.sync.dma_start(out=out_v[b][:, :, n0:n0 + 2 * P], in_=osb[:])
+            if i % 8 == 7:
+                b = i // 8
+                nc.sync.dma_start(out=out1_v[b:b + 1, :], in_=rz_all[0:1, b * HW:(b + 1) * HW])
+
+        with tc.manual_schedule():
+            mem_ss(0)
+            mem_ss(1)
+            mem_rsqrt(0)
+            xgram(0, ps_sim, "sim")
+            xdiag(0)
+            mem_rsqrt(1)
+            xrsqrt(0)
+            mem_scale(0)
+            xgram(1, ps_sim, "sim")
+            xdiag(1)
+            xrsqrt(1)
+            mem_scale(1)
+            mem_flip(0)
+            mem_evac(0)
+            mem_flip(1)
+            mem_quant1(0)
+            xbcast(0, ps_acc, "acc")
+            mem_evac(1)
+            xbcast(1, ps_bc, "bc")
+            xcopy(1)
+            mem_group2(0)
+            mem_group2(1)
+            for a in range(4):
+                xmul(1, a)
+            st[("fg", 0)] = work.tile([P, 512, 4], BF16, name="fg0", bufs=1, align_bytes=64)
+            xmul0(0)
+            mem_quant1(1)
+            xmul0(1)
+            xquant(0, 0, 1)
+            xquant(0, 1, 1)
+            mm1(0)
+            mm1(1)
+            rowmax(0)
+            rowmax(1)
+            xmul0(2)
+            xmul0(3)
+            xquant(0, 2, 1)
+            xquant(0, 3, 1)
+            for s in range(NT + 3):
+                if s - 3 >= 0:
+                    zbcast(s - 3)
+                    mm2(s - 3)
+                if s < NT:
+                    expo(s)
+                if s - 3 >= 0:
+                    zcopy(s - 3)
+                if s + 2 < NT:
+                    mm1(s + 2)
+                if s < NT:
+                    flip(s)
+                if s - 3 >= 0:
+                    finish(s - 3)
+                if s + 2 < NT:
+                    rowmax(s + 2)
+                if 0 <= s - 1 < NT:
+                    evac(s - 1)
+                    equant(s - 1)
+                    zchain(s - 1)
+                if s < 2:
+                    xgram(2 + s, ps_bc, "bc")
+                    xdiag(2 + s)
+                    xrsqrt(2 + s)
+                    mem_quant2(s)
+                if 3 <= s < 5:
+                    xbcast(s - 1, ps_bc, "bc")
+                    xcopy(s - 1)
+                    for a in range(4):
+                        xmul(s - 1, a)
+                for q in (1, 2, 3):
+                    if 0 <= s - (4 * q - 3) < 4:
+                        xquant(q, s - (4 * q - 3), 1)

@@ -23,7 +23,7 @@ def tile_memorybank2d_pa_kernel(tc, x, memory, out_0, out_1):
     nc = tc.nc
     with ExitStack() as ctx:
         keep = ctx.enter_context(tc.tile_pool(name="keep", bufs=1))
-        small = ctx.enter_context(tc.tile_pool(name="small", bufs=6))
+        small = ctx.enter_context(tc.tile_pool(name="small", bufs=8))
         work = ctx.enter_context(tc.tile_pool(name="work", bufs=4))
         ps_sim = ctx.enter_context(tc.psum_pool(name="ps_sim", bufs=4))
         ps_tp = ctx.enter_context(tc.psum_pool(name="ps_tp", bufs=2))
@@ -46,6 +46,8 @@ def tile_memorybank2d_pa_kernel(tc, x, memory, out_0, out_1):
         make_identity(nc, ident_f[:])
         nhalf = keep.tile([P, 4], F32)
         nc.vector.memset(nhalf[:], -0.5)
+        nones = keep.tile([P, 2], F32)
+        nc.vector.memset(nones[:], -1.0)
         warm = keep.tile([P, 1], F32)
         nc.vector.memset(warm[:], 0.0)
         warm2 = keep.tile([P, 1], F32)
@@ -73,13 +75,11 @@ def tile_memorybank2d_pa_kernel(tc, x, memory, out_0, out_1):
             st[("gram", q)] = gram
 
         def xdiag(q):
-            gram = st[("gram", q)]
+            dm = work.tile([P, 4, P], F32, name="dm", bufs=2)
+            nc.vector.tensor_tensor(out=dm[:], in0=st[("gram", q)][:],
+                                    in1=ident_f[:].unsqueeze(1).to_broadcast([P, 4, P]), op=ALU.mult)
             ssx = small.tile([P, 4], F32, name="ssx")
-            for a in range(4):
-                junkd = work.tile([P, P], F32, name="junkd")
-                nc.vector.scalar_tensor_tensor(
-                    out=junkd[:], in0=gram[:, a, :], scalar=1.0, in1=ident_f[:],
-                    op0=ALU.mult, op1=ALU.mult, accum_out=ssx[:, a:a + 1])
+            nc.vector.tensor_reduce(out=ssx[:], in_=dm[:], axis=AX.X, op=ALU.add)
             st[("ssx", q)] = ssx
 
         def xrsqrt(q):
@@ -93,29 +93,34 @@ def tile_memorybank2d_pa_kernel(tc, x, memory, out_0, out_1):
                 nc.tensor.matmul(rnb[:, a, :], lhsT=rnx[q][:, a:a + 1].to_broadcast([P, P]),
                                  rhs=ident_f[:], start=True, stop=True)
             st[("rnb", q)] = rnb
+            st[("fg", q)] = work.tile([P, 512, 4], BF16, name="fg", bufs=3, align_bytes=64)
 
-        def xview(q, a):
-            b, n0 = q // 2, (q % 2) * 512 + a * P
-            return x_sb[:, b, :, n0:n0 + P].rearrange("p t n -> p n t")
+        def xview(q, a0, na):
+            b, n0 = q // 2, (q % 2) * 512 + a0 * P
+            return x_sb[:, b, :, n0:n0 + na * P].rearrange("p t n -> p n t")
 
-        def xquant(q, a0, na):
-            fg = st[("fg", q)]
-            lo, hi = q * 512 + a0 * P, q * 512 + (a0 + na) * P
-            nc.vector.quantize_mx(
-                out=fc[:, lo:hi].bitcast(FP8X4), scales=fs[:, lo:hi],
-                in_=fg[:, a0 * P:(a0 + na) * P, :].rearrange("p n t -> p (n t)"))
+        def xmul_v(q, a0, na):
+            nc.vector.tensor_tensor(
+                out=st[("fg", q)][:, a0 * P:(a0 + na) * P, :], in0=xview(q, a0, na),
+                in1=st[("rnb", q)][:, a0:a0 + na, :].rearrange("p a n -> p (a n)").unsqueeze(2)
+                .to_broadcast([P, na * P, 4]), op=ALU.mult)
 
         def xcopy(q):
             rnbs = work.tile([P, 512], F32, name="rnbs", bufs=2)
             nc.scalar.copy(out=rnbs[:], in_=st[("rnb", q)][:].rearrange("p a n -> p (a n)"))
             st[("rnbs", q)] = rnbs
-            st[("fg", q)] = work.tile([P, 512, 4], BF16, name="fgl", bufs=2, align_bytes=64)
 
-        def xmul(q, a):
+        def xmul_g(q, a0, na):
             nc.gpsimd.tensor_tensor(
-                out=st[("fg", q)][:, a * P:(a + 1) * P, :], in0=xview(q, a),
-                in1=st[("rnbs", q)][:, a * P:(a + 1) * P].unsqueeze(2).to_broadcast([P, P, 4]),
+                out=st[("fg", q)][:, a0 * P:(a0 + na) * P, :], in0=xview(q, a0, na),
+                in1=st[("rnbs", q)][:, a0 * P:(a0 + na) * P].unsqueeze(2).to_broadcast([P, na * P, 4]),
                 op=ALU.mult)
+
+        def xquant(q, a0, na):
+            lo, hi = q * 512 + a0 * P, q * 512 + (a0 + na) * P
+            nc.vector.quantize_mx(
+                out=fc[:, lo:hi].bitcast(FP8X4), scales=fs[:, lo:hi],
+                in_=st[("fg", q)][:, a0 * P:(a0 + na) * P, :].rearrange("p n t -> p (n t)"))
 
         ss_all = keep.tile([P, 2, 8], F32)
         rn_all = keep.tile([P, 2, 8], F32)
@@ -183,11 +188,6 @@ def tile_memorybank2d_pa_kernel(tc, x, memory, out_0, out_1):
             nc.vector.quantize_mx(out=m2c[:, g, :].bitcast(FP8X4), scales=m2s[:, g, :],
                                   in_=g2[:, g].rearrange("p c j -> p (c j)"))
 
-        def xmul0(a):
-            nc.vector.tensor_tensor(
-                out=st[("fg", 0)][:, a * P:(a + 1) * P, :], in0=xview(0, a),
-                in1=st[("rnb", 0)][:, a, :].unsqueeze(2).to_broadcast([P, P, 4]), op=ALU.mult)
-
         rz_all = keep.tile([P, N], F32)
         out_v = out_0.rearrange("b (cc p) h w -> b p cc (h w)", p=P)
         out1_v = out_1.rearrange("b h w -> b (h w)")
@@ -217,20 +217,21 @@ def tile_memorybank2d_pa_kernel(tc, x, memory, out_0, out_1):
         def expo(i):
             sims = st[("sim", i)]
             e = work.tile([P, K], BF16, name="e")
-            z2 = small.tile([P, 2], F32, name="z2")
+            if i % 2 == 0:
+                st[("z4", i // 2)] = small.tile([P, 2, 2], F32, name="z4")
+            z4 = st[("z4", i // 2)]
             for h in range(2):
                 nc.scalar.activation(out=e[:, h * 512:(h + 1) * 512], in_=sims[h][:], func=ACT.Exp,
-                                     bias=st[("nmax", i)][:], scale=1.0, accum_out=z2[:, h:h + 1])
+                                     bias=st[("nmax", i)][:], scale=1.0, accum_out=z4[:, i % 2, h:h + 1])
             st[("e", i)] = e
-            st[("z2", i)] = z2
 
-        def zchain(i):
-            z2 = st[("z2", i)]
-            zs = small.tile([P, 1], F32, name="zs")
-            nc.vector.tensor_tensor(out=zs[:], in0=z2[:, 0:1], in1=z2[:, 1:2], op=ALU.add)
-            rz = small.tile([P, 1], F32, name="rz")
-            nc.vector.reciprocal(out=rz[:], in_=zs[:])
-            st[("rz", i)] = rz
+        def zchain(u):
+            z4 = st[("z4", u)]
+            zs = small.tile([P, 2], F32, name="zs")
+            nc.gpsimd.tensor_tensor(out=zs[:], in0=z4[:, :, 0], in1=z4[:, :, 1], op=ALU.add)
+            rz = small.tile([P, 2], F32, name="rz")
+            nc.gpsimd.tensor_tensor(out=rz[:], in0=zs[:], in1=nones[:], op=ALU.pow)
+            st[("rz", u)] = rz
 
         def flip(i):
             e = st[("e", i)]
@@ -240,32 +241,32 @@ def tile_memorybank2d_pa_kernel(tc, x, memory, out_0, out_1):
             st[("et", i)] = et
 
         def evac(i):
-            eg = work.tile([P, 2, P, 4], BF16, name="eg", align_bytes=64)
-            src = st[("et", i)][:].rearrange("p (g j) n -> p g n j", g=2)
-            if i % 4 == 3 and i > 3:
-                nc.vector.tensor_copy(out=eg[:], in_=src)
-            else:
-                nc.scalar.copy(out=eg[:], in_=src)
-            st[("eg", i)] = eg
+            if i % 2 == 0:
+                st[("eg", i // 2)] = work.tile([P, 2, 2, P, 4], BF16, name="eg", align_bytes=64)
+            nc.scalar.copy(out=st[("eg", i // 2)][:, i % 2],
+                           in_=st[("et", i)][:].rearrange("p (g j) n -> p g n j", g=2))
 
-        def equant(i):
-            ec = work.tile([P, 2 * P], U32, name="ec", align_bytes=64)
-            es = work.tile([P, 2 * P], U8, name="es", align_bytes=64)
+        def equant(u):
+            ec = work.tile([P, 4 * P], U32, name="ec", align_bytes=64)
+            es = work.tile([P, 4 * P], U8, name="es", align_bytes=64)
             nc.vector.quantize_mx(out=ec[:].bitcast(FP8X4), scales=es[:],
-                                  in_=st[("eg", i)][:].rearrange("p g n j -> p (g n j)"))
-            st[("ec", i)] = (ec, es)
+                                  in_=st[("eg", u)][:].rearrange("p i g n j -> p (i g n j)"))
+            st[("ec", u)] = (ec, es)
 
-        def zbcast(i):
-            zb = ps_bc.tile([P, P], F32, tag="bc", name="zb")
-            nc.tensor.matmul(zb[:], lhsT=st[("rz", i)][:, 0:1].to_broadcast([P, P]), rhs=ident_f[:],
-                             start=True, stop=True)
-            st[("zb", i)] = zb
+        def zbcast(u):
+            zb = ps_bc.tile([P, 2, P], F32, tag="bc", name="zb")
+            for w in range(2):
+                nc.tensor.matmul(zb[:, w, :], lhsT=st[("rz", u)][:, w:w + 1].to_broadcast([P, P]),
+                                 rhs=ident_f[:], start=True, stop=True)
+            st[("zb", u)] = zb
 
-        def zcopy(i):
-            nc.scalar.copy(out=rz_all[:, i * P:(i + 1) * P], in_=st[("zb", i)][:])
+        def zcopy(u):
+            nc.scalar.copy(out=rz_all[:, 2 * u * P:2 * (u + 1) * P],
+                           in_=st[("zb", u)][:].rearrange("p w n -> p (w n)"))
 
         def mm2(i):
-            ec, es = st[("ec", i)]
+            ec, es = st[("ec", i // 2)]
+            o = (i % 2) * 2 * P
             acc = ps_acc.tile([P, 4, P], F32, tag="acc", name="acc")
             for cc in range(4):
                 for g in range(2):
@@ -273,7 +274,8 @@ def tile_memorybank2d_pa_kernel(tc, x, memory, out_0, out_1):
                         out=acc[:, cc, :],
                         lhsT=m2c[:, g, cc * P:(cc + 1) * P].bitcast(FP8X4),
                         lhsT_scale=m2s[:, g, cc * P:(cc + 1) * P],
-                        rhs=ec[:, g * P:(g + 1) * P].bitcast(FP8X4), rhs_scale=es[:, g * P:(g + 1) * P],
+                        rhs=ec[:, o + g * P:o + (g + 1) * P].bitcast(FP8X4),
+                        rhs_scale=es[:, o + g * P:o + (g + 1) * P],
                         start=(g == 0), stop=(g == 1))
             st[("acc", i)] = acc
 
@@ -291,6 +293,8 @@ def tile_memorybank2d_pa_kernel(tc, x, memory, out_0, out_1):
             if i % 8 == 7:
                 b = i // 8
                 nc.sync.dma_start(out=out1_v[b:b + 1, :], in_=rz_all[0:1, b * HW:(b + 1) * HW])
+
+        LAG = 5
 
         with tc.manual_schedule():
             mem_ss(0)
@@ -315,52 +319,56 @@ def tile_memorybank2d_pa_kernel(tc, x, memory, out_0, out_1):
             xcopy(1)
             mem_group2(0)
             mem_group2(1)
-            for a in range(4):
-                xmul(1, a)
-            st[("fg", 0)] = work.tile([P, 512, 4], BF16, name="fg0", bufs=1, align_bytes=64)
-            xmul0(0)
+            xmul_g(1, 0, 2)
+            xmul_g(1, 2, 2)
+            xmul_v(0, 0, 2)
             mem_quant1(1)
-            xmul0(1)
-            xquant(0, 0, 1)
-            xquant(0, 1, 1)
+            xquant(0, 0, 2)
             mm1(0)
             mm1(1)
             rowmax(0)
             rowmax(1)
-            xmul0(2)
-            xmul0(3)
-            xquant(0, 2, 1)
-            xquant(0, 3, 1)
-            for s in range(NT + 3):
-                if s - 3 >= 0:
-                    zbcast(s - 3)
-                    mm2(s - 3)
+            xmul_v(0, 2, 2)
+            xquant(0, 2, 2)
+            for s in range(NT + LAG + 1):
+                i2 = s - LAG
+                if 0 <= i2 < NT:
+                    if i2 % 2 == 0:
+                        zbcast(i2 // 2)
+                    mm2(i2)
                 if s < NT:
                     expo(s)
-                if s - 3 >= 0:
-                    zcopy(s - 3)
+                    if s % 2 == 1:
+                        zchain(s // 2)
+                if 0 <= i2 < NT and i2 % 2 == 0:
+                    zcopy(i2 // 2)
                 if s + 2 < NT:
                     mm1(s + 2)
                 if s < NT:
                     flip(s)
-                if s - 3 >= 0:
-                    finish(s - 3)
+                if 0 <= i2 < NT:
+                    finish(i2)
                 if s + 2 < NT:
                     rowmax(s + 2)
                 if 0 <= s - 1 < NT:
                     evac(s - 1)
-                    equant(s - 1)
-                    zchain(s - 1)
+                    if s % 2 == 0:
+                        equant((s - 1) // 2)
+                if s == 0:
+                    xgram(2, ps_acc, "acc")
+                    xgram(3, ps_bc, "bc")
                 if s < 2:
-                    xgram(2 + s, ps_bc, "bc")
                     xdiag(2 + s)
                     xrsqrt(2 + s)
-                    mem_quant2(s)
-                if 3 <= s < 5:
-                    xbcast(s - 1, ps_bc, "bc")
-                    xcopy(s - 1)
-                    for a in range(4):
-                        xmul(s - 1, a)
-                for q in (1, 2, 3):
-                    if 0 <= s - (4 * q - 3) < 4:
-                        xquant(q, s - (4 * q - 3), 1)
+                if s % 2 == 1 and s < 12:
+                    xquant((s + 3) // 4, ((s + 3) % 4) // 2 * 2, 2)
+                if 2 <= s < 4:
+                    mem_quant2(s - 2)
+                if s == 3:
+                    xbcast(2, ps_acc, "acc")
+                    xcopy(2)
+                    xbcast(3, ps_bc, "bc")
+                    xcopy(3)
+                    for q in (2, 3):
+                        xmul_g(q, 0, 2)
+                        xmul_g(q, 2, 2)

@@ -48,6 +48,8 @@ def tile_memorybank2d_pa_kernel(tc, x, memory, out_0, out_1):
         nc.vector.memset(nhalf[:], -0.5)
         nones = keep.tile([P, 2], F32)
         nc.vector.memset(nones[:], -1.0)
+        ones3 = keep.tile([P, 4, P], F32)
+        nc.gpsimd.memset(ones3[:], 1.0)
         warm = keep.tile([P, 1], F32)
         nc.vector.memset(warm[:], 0.0)
         warm2 = keep.tile([P, 1], F32)
@@ -85,13 +87,15 @@ def tile_memorybank2d_pa_kernel(tc, x, memory, out_0, out_1):
         def xrsqrt(q):
             rq = keep.tile([P, 4], F32, name="rnx%d" % q)
             rsqrt_cols(rq[:], st[("ssx", q)][:], [P, 4], nhalf[:])
-            rnx[q] = rq
+            rrep = work.tile([P, 4, P], F32, name="rrep", bufs=2)
+            nc.gpsimd.tensor_tensor(out=rrep[:], in0=ones3[:],
+                                    in1=rq[:].unsqueeze(2).to_broadcast([P, 4, P]), op=ALU.mult)
+            rnx[q] = rrep
 
         def xbcast(q, pool, tag):
             rnb = pool.tile([P, 4, P], F32, tag=tag, name="rnb")
             for a in range(4):
-                nc.tensor.matmul(rnb[:, a, :], lhsT=rnx[q][:, a:a + 1].to_broadcast([P, P]),
-                                 rhs=ident_f[:], start=True, stop=True)
+                nc.tensor.transpose(rnb[:, a, :], rnx[q][:, a, :], ident_f[:])
             st[("rnb", q)] = rnb
             st[("fg", q)] = work.tile([P, 512, 4], BF16, name="fg", bufs=3, align_bytes=64)
 
@@ -231,7 +235,10 @@ def tile_memorybank2d_pa_kernel(tc, x, memory, out_0, out_1):
             nc.gpsimd.tensor_tensor(out=zs[:], in0=z4[:, :, 0], in1=z4[:, :, 1], op=ALU.add)
             rz = small.tile([P, 2], F32, name="rz")
             nc.gpsimd.tensor_tensor(out=rz[:], in0=zs[:], in1=nones[:], op=ALU.pow)
-            st[("rz", u)] = rz
+            zrep = work.tile([P, 2, P], F32, name="zrep")
+            nc.gpsimd.tensor_tensor(out=zrep[:], in0=ones3[:, 0:2, :],
+                                    in1=rz[:].unsqueeze(2).to_broadcast([P, 2, P]), op=ALU.mult)
+            st[("rz", u)] = zrep
 
         def flip(i):
             e = st[("e", i)]
@@ -256,8 +263,7 @@ def tile_memorybank2d_pa_kernel(tc, x, memory, out_0, out_1):
         def zbcast(u):
             zb = ps_bc.tile([P, 2, P], F32, tag="bc", name="zb")
             for w in range(2):
-                nc.tensor.matmul(zb[:, w, :], lhsT=st[("rz", u)][:, w:w + 1].to_broadcast([P, P]),
-                                 rhs=ident_f[:], start=True, stop=True)
+                nc.tensor.transpose(zb[:, w, :], st[("rz", u)][:, w, :], ident_f[:])
             st[("zb", u)] = zb
 
         def zcopy(u):

@@ -48,8 +48,6 @@ def tile_memorybank2d_pa_kernel(tc, x, memory, out_0, out_1):
         nc.vector.memset(nhalf[:], -0.5)
         nones = keep.tile([P, 2], F32)
         nc.vector.memset(nones[:], -1.0)
-        ones3 = keep.tile([P, 4, P], F32)
-        nc.gpsimd.memset(ones3[:], 1.0)
         warm = keep.tile([P, 1], F32)
         nc.vector.memset(warm[:], 0.0)
         warm2 = keep.tile([P, 1], F32)
@@ -87,15 +85,13 @@ def tile_memorybank2d_pa_kernel(tc, x, memory, out_0, out_1):
         def xrsqrt(q):
             rq = keep.tile([P, 4], F32, name="rnx%d" % q)
             rsqrt_cols(rq[:], st[("ssx", q)][:], [P, 4], nhalf[:])
-            rrep = work.tile([P, 4, P], F32, name="rrep", bufs=2)
-            nc.gpsimd.tensor_tensor(out=rrep[:], in0=ones3[:],
-                                    in1=rq[:].unsqueeze(2).to_broadcast([P, 4, P]), op=ALU.mult)
-            rnx[q] = rrep
+            rnx[q] = rq
 
         def xbcast(q, pool, tag):
             rnb = pool.tile([P, 4, P], F32, tag=tag, name="rnb")
             for a in range(4):
-                nc.tensor.transpose(rnb[:, a, :], rnx[q][:, a, :], ident_f[:])
+                nc.tensor.matmul(rnb[:, a, :], lhsT=rnx[q][:, a:a + 1].to_broadcast([P, P]),
+                                 rhs=ident_f[:], start=True, stop=True)
             st[("rnb", q)] = rnb
             st[("fg", q)] = work.tile([P, 512, 4], BF16, name="fg", bufs=3, align_bytes=64)
 
@@ -110,12 +106,12 @@ def tile_memorybank2d_pa_kernel(tc, x, memory, out_0, out_1):
                 .to_broadcast([P, na * P, 4]), op=ALU.mult)
 
         def xcopy(q):
-            rnbs = work.tile([P, 512], F32, name="rnbs", bufs=2)
+            rnbs = work.tile([P, 512], F32, name="rnbs", bufs=3)
             nc.scalar.copy(out=rnbs[:], in_=st[("rnb", q)][:].rearrange("p a n -> p (a n)"))
             st[("rnbs", q)] = rnbs
 
-        def xmul_g(q, a0, na):
-            nc.gpsimd.tensor_tensor(
+        def xmul_s(q, a0, na):
+            nc.vector.tensor_tensor(
                 out=st[("fg", q)][:, a0 * P:(a0 + na) * P, :], in0=xview(q, a0, na),
                 in1=st[("rnbs", q)][:, a0 * P:(a0 + na) * P].unsqueeze(2).to_broadcast([P, na * P, 4]),
                 op=ALU.mult)
@@ -185,8 +181,7 @@ def tile_memorybank2d_pa_kernel(tc, x, memory, out_0, out_1):
                 in_=g1[:, 4 * g:4 * g + 4].rearrange("p r k t -> p (r k t)"))
 
         def mem_group2(g):
-            nc.gpsimd.tensor_scalar(out=g2[:, g], in0=mn_sb[:, g].rearrange("p j c -> p c j"),
-                                    scalar1=1.0, scalar2=0.0, op0=ALU.mult, op1=ALU.add)
+            nc.scalar.copy(out=g2[:, g], in_=mn_sb[:, g].rearrange("p j c -> p c j"))
 
         def mem_quant2(g):
             nc.vector.quantize_mx(out=m2c[:, g, :].bitcast(FP8X4), scales=m2s[:, g, :],
@@ -235,10 +230,7 @@ def tile_memorybank2d_pa_kernel(tc, x, memory, out_0, out_1):
             nc.gpsimd.tensor_tensor(out=zs[:], in0=z4[:, :, 0], in1=z4[:, :, 1], op=ALU.add)
             rz = small.tile([P, 2], F32, name="rz")
             nc.gpsimd.tensor_tensor(out=rz[:], in0=zs[:], in1=nones[:], op=ALU.pow)
-            zrep = work.tile([P, 2, P], F32, name="zrep")
-            nc.gpsimd.tensor_tensor(out=zrep[:], in0=ones3[:, 0:2, :],
-                                    in1=rz[:].unsqueeze(2).to_broadcast([P, 2, P]), op=ALU.mult)
-            st[("rz", u)] = zrep
+            st[("rz", u)] = rz
 
         def flip(i):
             e = st[("e", i)]
@@ -263,7 +255,8 @@ def tile_memorybank2d_pa_kernel(tc, x, memory, out_0, out_1):
         def zbcast(u):
             zb = ps_bc.tile([P, 2, P], F32, tag="bc", name="zb")
             for w in range(2):
-                nc.tensor.transpose(zb[:, w, :], st[("rz", u)][:, w, :], ident_f[:])
+                nc.tensor.matmul(zb[:, w, :], lhsT=st[("rz", u)][:, w:w + 1].to_broadcast([P, P]),
+                                 rhs=ident_f[:], start=True, stop=True)
             st[("zb", u)] = zb
 
         def zcopy(u):
@@ -323,10 +316,6 @@ def tile_memorybank2d_pa_kernel(tc, x, memory, out_0, out_1):
             mem_evac(1)
             xbcast(1, ps_bc, "bc")
             xcopy(1)
-            mem_group2(0)
-            mem_group2(1)
-            xmul_g(1, 0, 2)
-            xmul_g(1, 2, 2)
             xmul_v(0, 0, 2)
             mem_quant1(1)
             xquant(0, 0, 2)
@@ -360,6 +349,10 @@ def tile_memorybank2d_pa_kernel(tc, x, memory, out_0, out_1):
                     evac(s - 1)
                     if s % 2 == 0:
                         equant((s - 1) // 2)
+                if s % 2 == 0 and s < 12:
+                    xmul_s((s + 4) // 4, ((s + 4) % 4) // 2 * 2, 2)
+                if s < 2:
+                    mem_group2(s)
                 if s == 0:
                     xgram(2, ps_acc, "acc")
                     xgram(3, ps_bc, "bc")
@@ -375,6 +368,3 @@ def tile_memorybank2d_pa_kernel(tc, x, memory, out_0, out_1):
                     xcopy(2)
                     xbcast(3, ps_bc, "bc")
                     xcopy(3)
-                    for q in (2, 3):
-                        xmul_g(q, 0, 2)
-                        xmul_g(q, 2, 2)

@@ -279,21 +279,17 @@ def tile_memorybank2d_pa_kernel(tc, x, memory, out_0, out_1):
             st[("acc", i)] = acc
 
         def finish(i):
-            if i % 2 == 0:
-                st["osb"] = work.tile([P, 4, 2 * P], F32, name="osb")
-            osb = st["osb"]
-            off = (i % 2) * P
+            osb = work.tile([P, 4, P], F32, name="osb", bufs=6)
             nc.vector.tensor_tensor(
-                out=osb[:, :, off:off + P], in0=st[("acc", i)][:],
+                out=osb[:], in0=st[("acc", i)][:],
                 in1=rz_all[:, i * P:(i + 1) * P].unsqueeze(1).to_broadcast([P, 4, P]), op=ALU.mult)
-            if i % 2 == 1:
-                b, n0 = i // 8, ((i - 1) % 8) * P
-                nc.sync.dma_start(out=out_v[b][:, :, n0:n0 + 2 * P], in_=osb[:])
+            b, n0 = i // 8, (i % 8) * P
+            nc.sync.dma_start(out=out_v[b][:, :, n0:n0 + P], in_=osb[:])
             if i % 8 == 7:
                 b = i // 8
                 nc.sync.dma_start(out=out1_v[b:b + 1, :], in_=rz_all[0:1, b * HW:(b + 1) * HW])
 
-        LAG = 5
+        LAG = 4
 
         with tc.manual_schedule():
             mem_ss(0)
@@ -363,7 +359,7 @@ def tile_memorybank2d_pa_kernel(tc, x, memory, out_0, out_1):
                     xquant((s + 3) // 4, ((s + 3) % 4) // 2 * 2, 2)
                 if 2 <= s < 4:
                     mem_quant2(s - 2)
-                if s == 3:
+                if s == 2:
                     xbcast(2, ps_acc, "acc")
                     xcopy(2)
                     xbcast(3, ps_bc, "bc")

@@ -279,19 +279,23 @@ def tile_memorybank2d_pa_kernel(tc, x, memory, out_0, out_1):
             st[("acc", i)] = acc
 
         def finish(i):
-            osb = work.tile([P, 4, P], F32, name="osb", bufs=6)
+            if i % 2 == 0:
+                st["osb"] = work.tile([P, 4, 2 * P], F32, name="osb")
+            osb = st["osb"]
+            off = (i % 2) * P
             nc.vector.tensor_tensor(
-                out=osb[:], in0=st[("acc", i)][:],
+                out=osb[:, :, off:off + P], in0=st[("acc", i)][:],
                 in1=rz_all[:, i * P:(i + 1) * P].unsqueeze(1).to_broadcast([P, 4, P]), op=ALU.mult)
-            b, n0 = i // 8, (i % 8) * P
-            nc.sync.dma_start(out=out_v[b][:, :, n0:n0 + P], in_=osb[:])
+            if i % 2 == 1:
+                b, n0 = i // 8, ((i - 1) % 8) * P
+                nc.sync.dma_start(out=out_v[b][:, :, n0:n0 + 2 * P], in_=osb[:])
             if i % 8 == 7:
                 b = i // 8
                 nc.sync.dma_start(out=out1_v[b:b + 1, :], in_=rz_all[0:1, b * HW:(b + 1) * HW])
 
-        LAG = 4
+        LAG = 5
 
-        with tc.manual_schedule():
+        for once in range(1):
             mem_ss(0)
             mem_ss(1)
             mem_rsqrt(0)
@@ -359,7 +363,7 @@ def tile_memorybank2d_pa_kernel(tc, x, memory, out_0, out_1):
                     xquant((s + 3) // 4, ((s + 3) % 4) // 2 * 2, 2)
                 if 2 <= s < 4:
                     mem_quant2(s - 2)
-                if s == 2:
+                if s == 3:
                     xbcast(2, ps_acc, "acc")
                     xcopy(2)
                     xbcast(3, ps_bc, "bc")

@@ -33,33 +33,25 @@ def tile_memorybank2d_pa_kernel(tc, x, memory, out_0, out_1):
         mem_sb = keep.tile([P, 2, 4, C], BF16)
         mem_v = memory.rearrange("(g p j) c -> g p j c", g=2, p=P, j=4)
         x_sb = keep.tile([P, B, 4, HW], BF16)
-        x_v = x.rearrange("b (t p) h w -> b p t (h w)", p=P)
+        x_v = x.rearrange("b (p t) h w -> b p t (h w)", t=4)
         nc.sync.dma_start(out=mem_sb[:, 0], in_=mem_v[0])
         nc.sync.dma_start(out=mem_sb[:, 1], in_=mem_v[1])
         nc.sync.dma_start(out=x_sb[:, 0, :, 0:512], in_=x_v[0][:, :, 0:512])
         nc.sync.dma_start(out=x_sb[:, 0, :, 512:1024], in_=x_v[0][:, :, 512:1024])
         nc.sync.dma_start(out=x_sb[:, 1], in_=x_v[1])
 
-        ident_bf = keep.tile([P, P], BF16)
-        make_identity(nc, ident_bf[:])
         ident_f = keep.tile([P, P], F32)
         make_identity(nc, ident_f[:])
-        nhalf = keep.tile([P, 4], F32)
-        nc.vector.memset(nhalf[:], -0.5)
+        ones_f = keep.tile([P, P], F32)
+        nc.gpsimd.memset(ones_f[:], 1.0)
         nones = keep.tile([P, 2], F32)
         nc.vector.memset(nones[:], -1.0)
         warm = keep.tile([P, 1], F32)
-        nc.vector.memset(warm[:], 0.0)
+        nc.vector.memset(warm[:], 1.0)
         warm2 = keep.tile([P, 1], F32)
-        nc.scalar.activation(out=warm2[:], in_=warm[:], func=ACT.Exp)
+        nc.scalar.activation(out=warm2[:], in_=warm[:], func=ACT.Abs_reciprocal_sqrt)
 
-        def rsqrt_cols(dst, src, shape, expo):
-            cl = small.tile(shape, F32, name="cl")
-            nc.gpsimd.tensor_scalar(out=cl[:], in0=src, scalar1=3.0e38, scalar2=1.0e-24,
-                                    op0=ALU.min, op1=ALU.max)
-            nc.gpsimd.tensor_tensor(out=dst, in0=cl[:], in1=expo, op=ALU.pow)
-
-        rnx = {}
+        rnx = keep.tile([P, N], F32)
         fc = keep.tile([P, N], U32, align_bytes=64)
         fs = keep.tile([P, N], U8, align_bytes=64)
         st = {}
@@ -76,45 +68,29 @@ def tile_memorybank2d_pa_kernel(tc, x, memory, out_0, out_1):
 
         def xdiag(q):
             dm = work.tile([P, 4, P], F32, name="dm", bufs=2)
-            nc.vector.tensor_tensor(out=dm[:], in0=st[("gram", q)][:],
-                                    in1=ident_f[:].unsqueeze(1).to_broadcast([P, 4, P]), op=ALU.mult)
-            ssx = small.tile([P, 4], F32, name="ssx")
-            nc.vector.tensor_reduce(out=ssx[:], in_=dm[:], axis=AX.X, op=ALU.add)
-            st[("ssx", q)] = ssx
-
-        def xrsqrt(q):
-            rq = keep.tile([P, 4], F32, name="rnx%d" % q)
-            rsqrt_cols(rq[:], st[("ssx", q)][:], [P, 4], nhalf[:])
-            rnx[q] = rq
+            nc.vector.scalar_tensor_tensor(
+                out=dm[:], in0=st[("gram", q)][:], scalar=1.0e-24,
+                in1=ident_f[:].unsqueeze(1).to_broadcast([P, 4, P]), op0=ALU.max, op1=ALU.mult)
+            st[("dm", q)] = dm
 
         def xbcast(q, pool, tag):
-            rnb = pool.tile([P, 4, P], F32, tag=tag, name="rnb")
-            for a in range(4):
-                nc.tensor.matmul(rnb[:, a, :], lhsT=rnx[q][:, a:a + 1].to_broadcast([P, P]),
-                                 rhs=ident_f[:], start=True, stop=True)
-            st[("rnb", q)] = rnb
-            st[("fg", q)] = work.tile([P, 512, 4], BF16, name="fg", bufs=3, align_bytes=64)
+            ssb = pool.tile([P, 512], F32, tag=tag, name="ssb")
+            nc.tensor.matmul(ssb[:], lhsT=ones_f[:], rhs=st[("dm", q)][:].rearrange("p a n -> p (a n)"),
+                             start=True, stop=True)
+            nc.scalar.activation(out=rnx[:, q * 512:(q + 1) * 512], in_=ssb[:],
+                                 func=ACT.Abs_reciprocal_sqrt)
 
         def xview(q, a0, na):
             b, n0 = q // 2, (q % 2) * 512 + a0 * P
             return x_sb[:, b, :, n0:n0 + na * P].rearrange("p t n -> p n t")
 
-        def xmul_v(q, a0, na):
+        def xmul(q, a0, na):
+            if a0 == 0:
+                st[("fg", q)] = work.tile([P, 512, 4], BF16, name="fg", bufs=3, align_bytes=64)
+            lo, hi = q * 512 + a0 * P, q * 512 + (a0 + na) * P
             nc.vector.tensor_tensor(
                 out=st[("fg", q)][:, a0 * P:(a0 + na) * P, :], in0=xview(q, a0, na),
-                in1=st[("rnb", q)][:, a0:a0 + na, :].rearrange("p a n -> p (a n)").unsqueeze(2)
-                .to_broadcast([P, na * P, 4]), op=ALU.mult)
-
-        def xcopy(q):
-            rnbs = work.tile([P, 512], F32, name="rnbs", bufs=3)
-            nc.scalar.copy(out=rnbs[:], in_=st[("rnb", q)][:].rearrange("p a n -> p (a n)"))
-            st[("rnbs", q)] = rnbs
-
-        def xmul_s(q, a0, na):
-            nc.vector.tensor_tensor(
-                out=st[("fg", q)][:, a0 * P:(a0 + na) * P, :], in0=xview(q, a0, na),
-                in1=st[("rnbs", q)][:, a0 * P:(a0 + na) * P].unsqueeze(2).to_broadcast([P, na * P, 4]),
-                op=ALU.mult)
+                in1=rnx[:, lo:hi].unsqueeze(2).to_broadcast([P, na * P, 4]), op=ALU.mult)
 
         def xquant(q, a0, na):
             lo, hi = q * 512 + a0 * P, q * 512 + (a0 + na) * P
@@ -125,7 +101,7 @@ def tile_memorybank2d_pa_kernel(tc, x, memory, out_0, out_1):
         ss_all = keep.tile([P, 2, 8], F32)
         rn_all = keep.tile([P, 2, 8], F32)
         mn_sb = keep.tile([P, 2, 4, C], BF16)
-        g1 = keep.tile([P, 8, P, 4], BF16, align_bytes=64)
+        g1 = keep.tile([P, 2, 2, P, 2, 4], BF16, align_bytes=64)
         m1c = keep.tile([P, K], U32, align_bytes=64)
         m1s = keep.tile([P, K], U8, align_bytes=64)
         g2 = keep.tile([P, 2, C, 4], BF16, align_bytes=64)
@@ -143,8 +119,11 @@ def tile_memorybank2d_pa_kernel(tc, x, memory, out_0, out_1):
                                      accum_out=ss_all[:, 1, 2 * g + jj:2 * g + jj + 1])
 
         def mem_rsqrt(g):
-            rsqrt_cols(rn_all[:, :, 2 * g:2 * g + 2], ss_all[:, :, 2 * g:2 * g + 2], [P, 2, 2],
-                       nhalf[:].rearrange("p (a b) -> p a b", a=2))
+            cl = small.tile([P, 2, 2], F32, name="cl")
+            nc.vector.tensor_scalar(out=cl[:], in0=ss_all[:, :, 2 * g:2 * g + 2], scalar1=1.0e-24,
+                                    scalar2=None, op0=ALU.max)
+            nc.scalar.activation(out=rn_all[:, :, 2 * g:2 * g + 2], in_=cl[:],
+                                 func=ACT.Abs_reciprocal_sqrt)
 
         def mem_scale(g):
             for j in range(4):
@@ -157,28 +136,29 @@ def tile_memorybank2d_pa_kernel(tc, x, memory, out_0, out_1):
                                          func=ACT.Copy, scale=rcol)
 
         def mem_flip(g):
-            for jp in range(2):
-                tp = ps_tp.tile([P, 2, 4, P], BF16, tag="tp", name="tpm")
-                for jj in range(2):
-                    for t in range(4):
-                        nc.tensor.transpose(tp[:, jj, t, :], mn_sb[:, g, 2 * jp + jj, t * P:(t + 1) * P],
-                                            ident_bf[:])
-                st[("tpm", g, jp)] = tp
+            for u in range(2):
+                tp = ps_tp.tile([P, 2, 2, P], F32, tag="tp", name="tpm")
+                for e in range(2):
+                    words = mn_sb[:, g, 2 * u + e, :].bitcast(F32)
+                    for w in range(2):
+                        nc.tensor.transpose(tp[:, e, w, :], words[:, w::2], ident_f[:])
+                st[("tpm", g, u)] = tp
 
         def mem_evac(g):
-            for jp in range(2):
-                r0 = 4 * g + 2 * jp
-                src = st[("tpm", g, jp)][:].rearrange("p r t k -> p r k t")
-                if jp == 0:
-                    nc.vector.tensor_copy(out=g1[:, r0:r0 + 2], in_=src)
+            for u in range(2):
+                src = st[("tpm", g, u)][:].rearrange("p e w q -> p q e w")
+                dst = g1[:, g, u].rearrange("p q e t -> p (q e t)").bitcast(F32).rearrange(
+                    "p (q e w) -> p q e w", e=2, w=2)
+                if u == 0:
+                    nc.vector.tensor_copy(out=dst, in_=src)
                 else:
-                    nc.scalar.copy(out=g1[:, r0:r0 + 2], in_=src)
+                    nc.scalar.copy(out=dst, in_=src)
 
         def mem_quant1(g):
             nc.vector.quantize_mx(
                 out=m1c[:, g * 512:(g + 1) * 512].bitcast(FP8X4),
                 scales=m1s[:, g * 512:(g + 1) * 512],
-                in_=g1[:, 4 * g:4 * g + 4].rearrange("p r k t -> p (r k t)"))
+                in_=g1[:, g].rearrange("p u q e t -> p (u q e t)"))
 
         def mem_group2(g):
             nc.scalar.copy(out=g2[:, g], in_=mn_sb[:, g].rearrange("p j c -> p c j"))
@@ -233,17 +213,18 @@ def tile_memorybank2d_pa_kernel(tc, x, memory, out_0, out_1):
             st[("rz", u)] = rz
 
         def flip(i):
-            e = st[("e", i)]
-            et = ps_tp.tile([P, 8, P], BF16, tag="tp", name="et")
-            for r in range(8):
-                nc.tensor.transpose(et[:, r, :], e[:, r * P:(r + 1) * P], ident_bf[:])
+            words = st[("e", i)][:].bitcast(F32)
+            et = ps_tp.tile([P, 4, P], F32, tag="tp", name="et")
+            for r in range(4):
+                nc.tensor.transpose(et[:, r, :], words[:, r * P:(r + 1) * P], ident_f[:])
             st[("et", i)] = et
 
         def evac(i):
             if i % 2 == 0:
                 st[("eg", i // 2)] = work.tile([P, 2, 2, P, 4], BF16, name="eg", align_bytes=64)
-            nc.scalar.copy(out=st[("eg", i // 2)][:, i % 2],
-                           in_=st[("et", i)][:].rearrange("p (g j) n -> p g n j", g=2))
+            dst = st[("eg", i // 2)][:, i % 2].rearrange("p g n t -> p (g n t)").bitcast(F32).rearrange(
+                "p (g n u) -> p g n u", g=2, u=2)
+            nc.scalar.copy(out=dst, in_=st[("et", i)][:].rearrange("p (g u) n -> p g n u", g=2))
 
         def equant(u):
             ec = work.tile([P, 4 * P], U32, name="ec", align_bytes=64)
@@ -299,31 +280,34 @@ def tile_memorybank2d_pa_kernel(tc, x, memory, out_0, out_1):
             mem_ss(0)
             mem_ss(1)
             mem_rsqrt(0)
+            mem_rsqrt(1)
             xgram(0, ps_sim, "sim")
             xdiag(0)
-            mem_rsqrt(1)
-            xrsqrt(0)
+            xbcast(0, ps_acc, "acc")
             mem_scale(0)
-            xgram(1, ps_sim, "sim")
-            xdiag(1)
-            xrsqrt(1)
-            mem_scale(1)
             mem_flip(0)
+            mem_scale(1)
             mem_evac(0)
             mem_flip(1)
             mem_quant1(0)
-            xbcast(0, ps_acc, "acc")
             mem_evac(1)
-            xbcast(1, ps_bc, "bc")
-            xcopy(1)
-            xmul_v(0, 0, 2)
+            xmul(0, 0, 2)
             mem_quant1(1)
             xquant(0, 0, 2)
+            for q in range(1, 4):
+                xgram(q, ps_sim, "sim")
+                xdiag(q)
+                if q % 2 == 1:
+                    xbcast(q, ps_bc, "bc")
+                else:
+                    xbcast(q, ps_acc, "acc")
+            warm3 = keep.tile([P, 1], F32)
+            nc.scalar.activation(out=warm3[:], in_=rnx[:, N - 1:N], func=ACT.Exp)
             mm1(0)
             mm1(1)
             rowmax(0)
             rowmax(1)
-            xmul_v(0, 2, 2)
+            xmul(0, 2, 2)
             xquant(0, 2, 2)
             for s in range(NT + LAG + 1):
                 i2 = s - LAG
@@ -350,21 +334,10 @@ def tile_memorybank2d_pa_kernel(tc, x, memory, out_0, out_1):
                     if s % 2 == 0:
                         equant((s - 1) // 2)
                 if s % 2 == 0 and s < 12:
-                    xmul_s((s + 4) // 4, ((s + 4) % 4) // 2 * 2, 2)
+                    xmul((s + 4) // 4, ((s + 4) % 4) // 2 * 2, 2)
                 if s < 2:
                     mem_group2(s)
-                if s == 0:
-                    xgram(2, ps_acc, "acc")
-                    xgram(3, ps_bc, "bc")
-                if s < 2:
-                    xdiag(2 + s)
-                    xrsqrt(2 + s)
                 if s % 2 == 1 and s < 12:
                     xquant((s + 3) // 4, ((s + 3) % 4) // 2 * 2, 2)
                 if 2 <= s < 4:
                     mem_quant2(s - 2)
-                if s == 3:
-                    xbcast(2, ps_acc, "acc")
-                    xcopy(2)
-                    xbcast(3, ps_bc, "bc")
-                    xcopy(3)

@@ -17,6 +17,7 @@ B, C, HW, K = 2, 512, 1024, 1024
 N = B * HW
 NT = N // P
 FLOPS = 2 * N * K * C * 2
+LAG = 4
 
 
 def tile_memorybank2d_pa_kernel(tc, x, memory, out_0, out_1):
@@ -149,10 +150,7 @@ def tile_memorybank2d_pa_kernel(tc, x, memory, out_0, out_1):
                 src = st[("tpm", g, u)][:].rearrange("p e w q -> p q e w")
                 dst = g1[:, g, u].rearrange("p q e t -> p (q e t)").bitcast(F32).rearrange(
                     "p (q e w) -> p q e w", e=2, w=2)
-                if u == 0:
-                    nc.vector.tensor_copy(out=dst, in_=src)
-                else:
-                    nc.scalar.copy(out=dst, in_=src)
+                nc.scalar.copy(out=dst, in_=src)
 
         def mem_quant1(g):
             nc.vector.quantize_mx(
@@ -226,18 +224,20 @@ def tile_memorybank2d_pa_kernel(tc, x, memory, out_0, out_1):
                 "p (g n u) -> p g n u", g=2, u=2)
             nc.scalar.copy(out=dst, in_=st[("et", i)][:].rearrange("p (g u) n -> p g n u", g=2))
 
-        def equant(u):
-            ec = work.tile([P, 4 * P], U32, name="ec", align_bytes=64)
-            es = work.tile([P, 4 * P], U8, name="es", align_bytes=64)
-            nc.vector.quantize_mx(out=ec[:].bitcast(FP8X4), scales=es[:],
-                                  in_=st[("eg", u)][:].rearrange("p i g n j -> p (i g n j)"))
-            st[("ec", u)] = (ec, es)
+        def equant(u, w0, nw):
+            if w0 == 0:
+                ec = work.tile([P, 4 * P], U32, name="ec", align_bytes=64)
+                es = work.tile([P, 4 * P], U8, name="es", align_bytes=64)
+                st[("ec", u)] = (ec, es)
+            ec, es = st[("ec", u)]
+            cols = slice(w0 * 2 * P, (w0 + nw) * 2 * P)
+            nc.vector.quantize_mx(out=ec[:, cols].bitcast(FP8X4), scales=es[:, cols],
+                                  in_=st[("eg", u)][:, w0:w0 + nw].rearrange("p i g n j -> p (i g n j)"))
 
         def zbcast(u):
             zb = ps_bc.tile([P, 2, P], F32, tag="bc", name="zb")
             for w in range(2):
-                nc.tensor.matmul(zb[:, w, :], lhsT=st[("rz", u)][:, w:w + 1].to_broadcast([P, P]),
-                                 rhs=ident_f[:], start=True, stop=True)
+                nc.tensor.transpose(zb[:, w, :], st[("rz", u)][:, w:w + 1].to_broadcast([P, P]), ident_f[:])
             st[("zb", u)] = zb
 
         def zcopy(u):
@@ -247,7 +247,10 @@ def tile_memorybank2d_pa_kernel(tc, x, memory, out_0, out_1):
         def mm2(i):
             ec, es = st[("ec", i // 2)]
             o = (i % 2) * 2 * P
-            acc = ps_acc.tile([P, 4, P], F32, tag="acc", name="acc")
+            if i < NT - LAG:
+                acc = ps_acc.tile([P, 4, P], F32, tag="acc", name="acc")
+            else:
+                acc = ps_sim.tile([P, 4, P], F32, tag="sim", name="acc")
             for cc in range(4):
                 for g in range(2):
                     nc.tensor.matmul_mx(
@@ -264,17 +267,20 @@ def tile_memorybank2d_pa_kernel(tc, x, memory, out_0, out_1):
                 st["osb"] = work.tile([P, 4, 2 * P], F32, name="osb")
             osb = st["osb"]
             off = (i % 2) * P
-            nc.vector.tensor_tensor(
-                out=osb[:, :, off:off + P], in0=st[("acc", i)][:],
-                in1=rz_all[:, i * P:(i + 1) * P].unsqueeze(1).to_broadcast([P, 4, P]), op=ALU.mult)
-            if i % 2 == 1:
-                b, n0 = i // 8, ((i - 1) % 8) * P
-                nc.sync.dma_start(out=out_v[b][:, :, n0:n0 + 2 * P], in_=osb[:])
+            b, n0 = i // 8, (i % 8) * P
+            step = 2 if i == NT - 1 else 4
+            for c0 in range(0, 4, step):
+                nc.vector.tensor_tensor(
+                    out=osb[:, c0:c0 + step, off:off + P], in0=st[("acc", i)][:, c0:c0 + step],
+                    in1=rz_all[:, i * P:(i + 1) * P].unsqueeze(1).to_broadcast([P, step, P]), op=ALU.mult)
+                if i >= NT - 2:
+                    nc.sync.dma_start(out=out_v[b][:, c0:c0 + step, n0:n0 + P],
+                                      in_=osb[:, c0:c0 + step, off:off + P])
+            if i % 2 == 1 and i < NT - 2:
+                nc.sync.dma_start(out=out_v[b][:, :, n0 - P:n0 + P], in_=osb[:])
             if i % 8 == 7:
                 b = i // 8
                 nc.sync.dma_start(out=out1_v[b:b + 1, :], in_=rz_all[0:1, b * HW:(b + 1) * HW])
-
-        LAG = 5
 
         for once in range(1):
             mem_ss(0)
@@ -331,8 +337,10 @@ def tile_memorybank2d_pa_kernel(tc, x, memory, out_0, out_1):
                     rowmax(s + 2)
                 if 0 <= s - 1 < NT:
                     evac(s - 1)
-                    if s % 2 == 0:
-                        equant((s - 1) // 2)
+                    if s >= NT - 1:
+                        equant((s - 1) // 2, (s - 1) % 2, 1)
+                    elif s % 2 == 0:
+                        equant((s - 1) // 2, 0, 2)
                 if s % 2 == 0 and s < 12:
                     xmul((s + 4) // 4, ((s + 4) % 4) // 2 * 2, 2)
                 if s < 2:

@@ -17,7 +17,8 @@ B, C, HW, K = 2, 512, 1024, 1024
 N = B * HW
 NT = N // P
 FLOPS = 2 * N * K * C * 2
-LAG = 4
+ML = 3
+FL = 4
 
 
 def tile_memorybank2d_pa_kernel(tc, x, memory, out_0, out_1):
@@ -28,8 +29,9 @@ def tile_memorybank2d_pa_kernel(tc, x, memory, out_0, out_1):
         work = ctx.enter_context(tc.tile_pool(name="work", bufs=4))
         ps_sim = ctx.enter_context(tc.psum_pool(name="ps_sim", bufs=4))
         ps_tp = ctx.enter_context(tc.psum_pool(name="ps_tp", bufs=2))
-        ps_acc = ctx.enter_context(tc.psum_pool(name="ps_acc", bufs=1))
-        ps_bc = ctx.enter_context(tc.psum_pool(name="ps_bc", bufs=1))
+        ps_acc = ctx.enter_context(tc.psum_pool(name="ps_acc", bufs=2))
+        ctx.enter_context(tc.manual_schedule())
+        st = {}
 
         mem_sb = keep.tile([P, 2, 4, C], BF16)
         mem_v = memory.rearrange("(g p j) c -> g p j c", g=2, p=P, j=4)
@@ -45,6 +47,8 @@ def tile_memorybank2d_pa_kernel(tc, x, memory, out_0, out_1):
         make_identity(nc, ident_f[:])
         ones_f = keep.tile([P, P], F32)
         nc.gpsimd.memset(ones_f[:], 1.0)
+        nhalf = keep.tile([P, 4], F32)
+        nc.gpsimd.memset(nhalf[:], -0.5)
         nones = keep.tile([P, 2], F32)
         nc.vector.memset(nones[:], -1.0)
         warm = keep.tile([P, 1], F32)
@@ -55,49 +59,74 @@ def tile_memorybank2d_pa_kernel(tc, x, memory, out_0, out_1):
         rnx = keep.tile([P, N], F32)
         fc = keep.tile([P, N], U32, align_bytes=64)
         fs = keep.tile([P, N], U8, align_bytes=64)
-        st = {}
 
-        def xgram(q, pool, tag):
-            b, n0 = q // 2, (q % 2) * 512
-            gram = pool.tile([P, 4, P], F32, tag=tag, name="gram")
-            for a in range(4):
-                cols = slice(n0 + a * P, n0 + (a + 1) * P)
+        def xgram(i0, n, pool, tag):
+            gram = pool.tile([P, n, P], F32, tag=tag, name="gram")
+            for a in range(n):
+                b, n0 = (i0 + a) // 8, (i0 + a) % 8 * P
                 for t in range(4):
-                    nc.tensor.matmul(gram[:, a, :], lhsT=x_sb[:, b, t, cols], rhs=x_sb[:, b, t, cols],
-                                     start=(t == 0), stop=(t == 3))
-            st[("gram", q)] = gram
+                    nc.tensor.matmul(gram[:, a, :], lhsT=x_sb[:, b, t, n0:n0 + P],
+                                     rhs=x_sb[:, b, t, n0:n0 + P], start=(t == 0), stop=(t == 3))
+            st[("gram", i0)] = gram
 
-        def xdiag(q):
-            dm = work.tile([P, 4, P], F32, name="dm", bufs=2)
+        def xdiag(i0, n):
+            dm = work.tile([P, n, P], F32, name="dm")
             nc.vector.scalar_tensor_tensor(
-                out=dm[:], in0=st[("gram", q)][:], scalar=1.0e-24,
-                in1=ident_f[:].unsqueeze(1).to_broadcast([P, 4, P]), op0=ALU.max, op1=ALU.mult)
-            st[("dm", q)] = dm
+                out=dm[:], in0=st[("gram", i0)][:], scalar=1.0e-24,
+                in1=ident_f[:].unsqueeze(1).to_broadcast([P, n, P]), op0=ALU.max, op1=ALU.mult)
+            st[("dm", i0)] = dm
 
-        def xbcast(q, pool, tag):
-            ssb = pool.tile([P, 512], F32, tag=tag, name="ssb")
-            nc.tensor.matmul(ssb[:], lhsT=ones_f[:], rhs=st[("dm", q)][:].rearrange("p a n -> p (a n)"),
+        def xspread(i0, n, pool, tag):
+            ssb = pool.tile([P, n * P], F32, tag=tag, name="ssb")
+            nc.tensor.matmul(ssb[:], lhsT=ones_f[:], rhs=st[("dm", i0)][:].rearrange("p a n -> p (a n)"),
                              start=True, stop=True)
-            nc.scalar.activation(out=rnx[:, q * 512:(q + 1) * 512], in_=ssb[:],
+            st[("ssb", i0)] = ssb
+
+        def xars(i0, n):
+            nc.scalar.activation(out=rnx[:, i0 * P:(i0 + n) * P], in_=st[("ssb", i0)][:],
                                  func=ACT.Abs_reciprocal_sqrt)
 
-        def xview(q, a0, na):
-            b, n0 = q // 2, (q % 2) * 512 + a0 * P
-            return x_sb[:, b, :, n0:n0 + na * P].rearrange("p t n -> p n t")
+        def xcols(i0, pool, tag):
+            ssc = pool.tile([P, 4], F32, tag=tag, name="ssc")
+            for a in range(4):
+                nc.tensor.matmul(ssc[:, a:a + 1], lhsT=st[("dm", i0)][:, a, :], rhs=ones_f[:, 0:1],
+                                 start=True, stop=True)
+            st[("ssc", i0)] = ssc
 
-        def xmul(q, a0, na):
-            if a0 == 0:
-                st[("fg", q)] = work.tile([P, 512, 4], BF16, name="fg", bufs=3, align_bytes=64)
-            lo, hi = q * 512 + a0 * P, q * 512 + (a0 + na) * P
+        def xcols_ars(i0):
+            rq = keep.tile([P, 4], F32, name="rnq%d" % i0)
+            nc.scalar.activation(out=rq[:], in_=st[("ssc", i0)][:], func=ACT.Abs_reciprocal_sqrt)
+            st[("rq", i0)] = rq
+
+        def xcols_pow(i0):
+            sscs = small.tile([P, 4], F32, name="sscs")
+            nc.scalar.copy(out=sscs[:], in_=st[("ssc", i0)][:])
+            rq = keep.tile([P, 4], F32, name="rnq%d" % i0)
+            nc.gpsimd.tensor_tensor(out=rq[:], in0=sscs[:], in1=nhalf[:], op=ALU.pow)
+            st[("rq", i0)] = rq
+
+        def xcast(i0, pool, tag):
+            rnb = pool.tile([P, 4, P], F32, tag=tag, name="rnb")
+            for a in range(4):
+                nc.tensor.transpose(rnb[:, a, :], st[("rq", i0)][:, a:a + 1].to_broadcast([P, P]), ident_f[:])
+            st[("rnb", i0)] = rnb
+
+        def xcopy(i0):
+            nc.scalar.copy(out=rnx[:, i0 * P:(i0 + 4) * P],
+                           in_=st[("rnb", i0)][:].rearrange("p a n -> p (a n)"))
+
+        def xmul(i0, n):
+            fg = work.tile([P, n * P, 4], BF16, name="fg", align_bytes=64)
+            b, n0 = i0 // 8, i0 % 8 * P
             nc.vector.tensor_tensor(
-                out=st[("fg", q)][:, a0 * P:(a0 + na) * P, :], in0=xview(q, a0, na),
-                in1=rnx[:, lo:hi].unsqueeze(2).to_broadcast([P, na * P, 4]), op=ALU.mult)
+                out=fg[:], in0=x_sb[:, b, :, n0:n0 + n * P].rearrange("p t n -> p n t"),
+                in1=rnx[:, i0 * P:(i0 + n) * P].unsqueeze(2).to_broadcast([P, n * P, 4]), op=ALU.mult)
+            st[("fg", i0)] = fg
 
-        def xquant(q, a0, na):
-            lo, hi = q * 512 + a0 * P, q * 512 + (a0 + na) * P
-            nc.vector.quantize_mx(
-                out=fc[:, lo:hi].bitcast(FP8X4), scales=fs[:, lo:hi],
-                in_=st[("fg", q)][:, a0 * P:(a0 + na) * P, :].rearrange("p n t -> p (n t)"))
+        def xquant(i0, n):
+            cols = slice(i0 * P, (i0 + n) * P)
+            nc.vector.quantize_mx(out=fc[:, cols].bitcast(FP8X4), scales=fs[:, cols],
+                                  in_=st[("fg", i0)][:].rearrange("p n t -> p (n t)"))
 
         ss_all = keep.tile([P, 2, 8], F32)
         rn_all = keep.tile([P, 2, 8], F32)
@@ -109,47 +138,51 @@ def tile_memorybank2d_pa_kernel(tc, x, memory, out_0, out_1):
         m2c = keep.tile([P, 2, C], U32, align_bytes=64)
         m2s = keep.tile([P, 2, C], U8, align_bytes=64)
 
-        def mem_ss(g):
-            for jj in range(2):
-                junkv = work.tile([P, C], F32, name="junkv")
-                nc.vector.scalar_tensor_tensor(
-                    out=junkv[:], in0=mem_sb[:, g, jj, :], scalar=1.0, in1=mem_sb[:, g, jj, :],
-                    op0=ALU.mult, op1=ALU.mult, accum_out=ss_all[:, 0, 2 * g + jj:2 * g + jj + 1])
-                junks = work.tile([P, C], F32, name="junks")
-                nc.scalar.activation(out=junks[:], in_=mem_sb[:, g, 2 + jj, :], func=ACT.Square,
-                                     accum_out=ss_all[:, 1, 2 * g + jj:2 * g + jj + 1])
+        def mem_ss_v(g, jj):
+            junkv = work.tile([P, C], F32, name="junkv")
+            nc.vector.scalar_tensor_tensor(
+                out=junkv[:], in0=mem_sb[:, g, jj, :], scalar=1.0, in1=mem_sb[:, g, jj, :],
+                op0=ALU.mult, op1=ALU.mult, accum_out=ss_all[:, 0, 2 * g + jj:2 * g + jj + 1])
 
-        def mem_rsqrt(g):
+        def mem_ss_s(g, jj):
+            junks = work.tile([P, C], F32, name="junks")
+            nc.scalar.activation(out=junks[:], in_=mem_sb[:, g, 2 + jj, :], func=ACT.Square,
+                                 accum_out=ss_all[:, 1, 2 * g + jj:2 * g + jj + 1])
+
+        def mem_clamp(g):
             cl = small.tile([P, 2, 2], F32, name="cl")
             nc.vector.tensor_scalar(out=cl[:], in0=ss_all[:, :, 2 * g:2 * g + 2], scalar1=1.0e-24,
                                     scalar2=None, op0=ALU.max)
-            nc.scalar.activation(out=rn_all[:, :, 2 * g:2 * g + 2], in_=cl[:],
+            st[("cl", g)] = cl
+
+        def mem_ars(g):
+            nc.scalar.activation(out=rn_all[:, :, 2 * g:2 * g + 2], in_=st[("cl", g)][:],
                                  func=ACT.Abs_reciprocal_sqrt)
 
-        def mem_scale(g):
-            for j in range(4):
-                rcol = rn_all[:, j // 2, 2 * g + j % 2:2 * g + j % 2 + 1]
-                if j < 3:
-                    nc.vector.tensor_scalar(out=mn_sb[:, g, j, :], in0=mem_sb[:, g, j, :],
-                                            scalar1=rcol, scalar2=None, op0=ALU.mult)
-                else:
-                    nc.scalar.activation(out=mn_sb[:, g, j, :], in_=mem_sb[:, g, j, :],
-                                         func=ACT.Copy, scale=rcol)
+        def mem_scale(g, j, eng):
+            rcol = rn_all[:, j // 2, 2 * g + j % 2:2 * g + j % 2 + 1]
+            if eng == "V":
+                nc.vector.tensor_scalar(out=mn_sb[:, g, j, :], in0=mem_sb[:, g, j, :],
+                                        scalar1=rcol, scalar2=None, op0=ALU.mult)
+            else:
+                nc.scalar.activation(out=mn_sb[:, g, j, :], in_=mem_sb[:, g, j, :],
+                                     func=ACT.Copy, scale=rcol)
 
-        def mem_flip(g):
-            for u in range(2):
-                tp = ps_tp.tile([P, 2, 2, P], F32, tag="tp", name="tpm")
-                for e in range(2):
-                    words = mn_sb[:, g, 2 * u + e, :].bitcast(F32)
-                    for w in range(2):
-                        nc.tensor.transpose(tp[:, e, w, :], words[:, w::2], ident_f[:])
-                st[("tpm", g, u)] = tp
+        def mem_flip(g, u):
+            tp = ps_tp.tile([P, 2, 2, P], F32, tag="tp", name="tpm")
+            for e in range(2):
+                words = mn_sb[:, g, 2 * u + e, :].bitcast(F32)
+                for w in range(2):
+                    nc.tensor.transpose(tp[:, e, w, :], words[:, w::2], ident_f[:])
+            st[("tpm", g, u)] = tp
 
-        def mem_evac(g):
-            for u in range(2):
-                src = st[("tpm", g, u)][:].rearrange("p e w q -> p q e w")
-                dst = g1[:, g, u].rearrange("p q e t -> p (q e t)").bitcast(F32).rearrange(
-                    "p (q e w) -> p q e w", e=2, w=2)
+        def mem_evac(g, u, eng):
+            src = st[("tpm", g, u)][:].rearrange("p e w q -> p q e w")
+            dst = g1[:, g, u].rearrange("p q e t -> p (q e t)").bitcast(F32).rearrange(
+                "p (q e w) -> p q e w", e=2, w=2)
+            if eng == "V":
+                nc.vector.tensor_copy(out=dst, in_=src)
+            else:
                 nc.scalar.copy(out=dst, in_=src)
 
         def mem_quant1(g):
@@ -158,8 +191,13 @@ def tile_memorybank2d_pa_kernel(tc, x, memory, out_0, out_1):
                 scales=m1s[:, g * 512:(g + 1) * 512],
                 in_=g1[:, g].rearrange("p u q e t -> p (u q e t)"))
 
-        def mem_group2(g):
-            nc.scalar.copy(out=g2[:, g], in_=mn_sb[:, g].rearrange("p j c -> p c j"))
+        def mem_group2(g, c0, eng):
+            dst = g2[:, g, c0:c0 + P]
+            src = mn_sb[:, g, :, c0:c0 + P].rearrange("p j c -> p c j")
+            if eng == "V":
+                nc.vector.tensor_copy(out=dst, in_=src)
+            else:
+                nc.scalar.copy(out=dst, in_=src)
 
         def mem_quant2(g):
             nc.vector.quantize_mx(out=m2c[:, g, :].bitcast(FP8X4), scales=m2s[:, g, :],
@@ -182,24 +220,26 @@ def tile_memorybank2d_pa_kernel(tc, x, memory, out_0, out_1):
             st[("sim", i)] = sims
 
         def rowmax(i):
-            sims = st[("sim", i)]
             nm2 = small.tile([P, 2], F32, name="nm2")
             for h in range(2):
-                nc.vector.tensor_reduce(out=nm2[:, h:h + 1], in_=sims[h][:], axis=AX.X, op=ALU.max,
-                                        negate=True)
-            nmax = small.tile([P, 1], F32, name="nmax")
-            nc.vector.tensor_tensor(out=nmax[:], in0=nm2[:, 0:1], in1=nm2[:, 1:2], op=ALU.min)
-            st[("nmax", i)] = nmax
+                nc.vector.tensor_reduce(out=nm2[:, h:h + 1], in_=st[("sim", i)][h][:], axis=AX.X,
+                                        op=ALU.max, negate=True)
+            st[("nm2", i)] = nm2
+
+        def nmax(i):
+            nm2 = st[("nm2", i)]
+            nm = small.tile([P, 1], F32, name="nm")
+            nc.vector.tensor_tensor(out=nm[:], in0=nm2[:, 0:1], in1=nm2[:, 1:2], op=ALU.min)
+            st[("nm", i)] = nm
 
         def expo(i):
-            sims = st[("sim", i)]
             e = work.tile([P, K], BF16, name="e")
             if i % 2 == 0:
                 st[("z4", i // 2)] = small.tile([P, 2, 2], F32, name="z4")
             z4 = st[("z4", i // 2)]
             for h in range(2):
-                nc.scalar.activation(out=e[:, h * 512:(h + 1) * 512], in_=sims[h][:], func=ACT.Exp,
-                                     bias=st[("nmax", i)][:], scale=1.0, accum_out=z4[:, i % 2, h:h + 1])
+                nc.scalar.activation(out=e[:, h * 512:(h + 1) * 512], in_=st[("sim", i)][h][:], func=ACT.Exp,
+                                     bias=st[("nm", i)][:], scale=1.0, accum_out=z4[:, i % 2, h:h + 1])
             st[("e", i)] = e
 
         def zchain(u):
@@ -234,8 +274,8 @@ def tile_memorybank2d_pa_kernel(tc, x, memory, out_0, out_1):
             nc.vector.quantize_mx(out=ec[:, cols].bitcast(FP8X4), scales=es[:, cols],
                                   in_=st[("eg", u)][:, w0:w0 + nw].rearrange("p i g n j -> p (i g n j)"))
 
-        def zbcast(u):
-            zb = ps_bc.tile([P, 2, P], F32, tag="bc", name="zb")
+        def zcast(u):
+            zb = ps_tp.tile([P, 2, P], F32, tag="tp", name="zb")
             for w in range(2):
                 nc.tensor.transpose(zb[:, w, :], st[("rz", u)][:, w:w + 1].to_broadcast([P, P]), ident_f[:])
             st[("zb", u)] = zb
@@ -247,7 +287,7 @@ def tile_memorybank2d_pa_kernel(tc, x, memory, out_0, out_1):
         def mm2(i):
             ec, es = st[("ec", i // 2)]
             o = (i % 2) * 2 * P
-            if i < NT - LAG:
+            if i < NT - ML - 1:
                 acc = ps_acc.tile([P, 4, P], F32, tag="acc", name="acc")
             else:
                 acc = ps_sim.tile([P, 4, P], F32, tag="sim", name="acc")
@@ -279,73 +319,134 @@ def tile_memorybank2d_pa_kernel(tc, x, memory, out_0, out_1):
             if i % 2 == 1 and i < NT - 2:
                 nc.sync.dma_start(out=out_v[b][:, :, n0 - P:n0 + P], in_=osb[:])
             if i % 8 == 7:
-                b = i // 8
                 nc.sync.dma_start(out=out1_v[b:b + 1, :], in_=rz_all[0:1, b * HW:(b + 1) * HW])
 
-        for once in range(1):
-            mem_ss(0)
-            mem_ss(1)
-            mem_rsqrt(0)
-            mem_rsqrt(1)
-            xgram(0, ps_sim, "sim")
-            xdiag(0)
-            xbcast(0, ps_acc, "acc")
-            mem_scale(0)
-            mem_flip(0)
-            mem_scale(1)
-            mem_evac(0)
-            mem_flip(1)
-            mem_quant1(0)
-            mem_evac(1)
-            xmul(0, 0, 2)
-            mem_quant1(1)
-            xquant(0, 0, 2)
-            for q in range(1, 4):
-                xgram(q, ps_sim, "sim")
-                xdiag(q)
-                if q % 2 == 1:
-                    xbcast(q, ps_bc, "bc")
-                else:
-                    xbcast(q, ps_acc, "acc")
-            warm3 = keep.tile([P, 1], F32)
-            nc.scalar.activation(out=warm3[:], in_=rnx[:, N - 1:N], func=ACT.Exp)
-            mm1(0)
-            mm1(1)
-            rowmax(0)
-            rowmax(1)
-            xmul(0, 2, 2)
-            xquant(0, 2, 2)
-            for s in range(NT + LAG + 1):
-                i2 = s - LAG
-                if 0 <= i2 < NT:
-                    if i2 % 2 == 0:
-                        zbcast(i2 // 2)
-                    mm2(i2)
-                if s < NT:
-                    expo(s)
-                    if s % 2 == 1:
-                        zchain(s // 2)
-                if 0 <= i2 < NT and i2 % 2 == 0:
-                    zcopy(i2 // 2)
-                if s + 2 < NT:
-                    mm1(s + 2)
-                if s < NT:
-                    flip(s)
-                if 0 <= i2 < NT:
-                    finish(i2)
-                if s + 2 < NT:
-                    rowmax(s + 2)
-                if 0 <= s - 1 < NT:
-                    evac(s - 1)
-                    if s >= NT - 1:
-                        equant((s - 1) // 2, (s - 1) % 2, 1)
-                    elif s % 2 == 0:
-                        equant((s - 1) // 2, 0, 2)
-                if s % 2 == 0 and s < 12:
-                    xmul((s + 4) // 4, ((s + 4) % 4) // 2 * 2, 2)
-                if s < 2:
-                    mem_group2(s)
-                if s % 2 == 1 and s < 12:
-                    xquant((s + 3) // 4, ((s + 3) % 4) // 2 * 2, 2)
-                if 2 <= s < 4:
-                    mem_quant2(s - 2)
+        mem_ss_v(0, 0)
+        mem_ss_s(0, 0)
+        mem_ss_v(0, 1)
+        mem_ss_s(0, 1)
+        mem_ss_v(1, 0)
+        mem_ss_s(1, 0)
+        mem_clamp(0)
+        mem_ars(0)
+        mem_ss_v(1, 1)
+        mem_ss_s(1, 1)
+        xgram(0, 2, ps_acc, "acc")
+        for j in range(4):
+            mem_scale(0, j, "V")
+        mem_flip(0, 0)
+        mem_flip(0, 1)
+        mem_clamp(1)
+        xdiag(0, 2)
+        mem_ars(1)
+        xspread(0, 2, ps_acc, "acc")
+        for j in range(4):
+            mem_scale(1, j, "V")
+        mem_evac(0, 0, "S")
+        mem_evac(0, 1, "S")
+        mem_flip(1, 0)
+        mem_flip(1, 1)
+        xars(0, 2)
+        mem_group2(0, 0, "V")
+        mem_group2(0, P, "V")
+        mem_group2(0, 2 * P, "V")
+        xgram(2, 2, ps_sim, "sim")
+        xgram(4, 4, ps_sim, "sim")
+        mem_quant1(0)
+        xmul(0, 1)
+        mem_evac(1, 0, "S")
+        xdiag(2, 2)
+        mem_evac(1, 1, "V")
+        mem_group2(0, 3 * P, "S")
+        mem_group2(1, 0, "S")
+        xquant(0, 1)
+        xspread(2, 2, ps_acc, "acc")
+        xdiag(4, 4)
+        mem_quant1(1)
+        xmul(1, 1)
+        mm1(0)
+        xcols(4, ps_acc, "acc")
+        xars(2, 2)
+        mem_group2(1, P, "S")
+        xcols_ars(4)
+        warm3 = keep.tile([P, 1], F32)
+        nc.scalar.activation(out=warm3[:], in_=st[("rq", 4)][:, 0:1], func=ACT.Exp)
+        mem_group2(1, 2 * P, "S")
+        xgram(8, 4, ps_tp, "tp")
+        rowmax(0)
+        xquant(1, 1)
+        nmax(0)
+        mm1(1)
+        xcast(4, ps_acc, "acc")
+        xgram(12, 4, ps_tp, "tp")
+        xmul(2, 1)
+        mem_quant2(0)
+        rowmax(1)
+        xquant(2, 1)
+        nmax(1)
+        xmul(3, 1)
+        xdiag(8, 4)
+        xcopy(4)
+        for s in range(NT):
+            expo(s)
+            if s % 2 == 1:
+                zchain(s // 2)
+            if s >= 1:
+                evac(s - 1)
+            if s >= 4 and s % 2 == 0:
+                zcopy((s - 4) // 2)
+            if s == 0:
+                mem_group2(1, 3 * P, "S")
+                xcols(8, ps_acc, "acc")
+            if s + 2 < NT:
+                mm1(s + 2)
+                flip(s)
+            if s == 1:
+                xcols_pow(8)
+                xcols(12, ps_acc, "acc")
+            if s == 2:
+                xcols_pow(12)
+                xcast(8, ps_acc, "acc")
+            if s == 3:
+                xcopy(8)
+                xcast(12, ps_acc, "acc")
+            if s == 4:
+                xcopy(12)
+            if s >= 3 and s % 2 == 1 and s + 2 < NT:
+                equant((s - 3) // 2, 0, 2)
+            if s % 2 == 0 and s < 12:
+                xmul(s + 4, 2)
+            if s + 2 < NT:
+                rowmax(s + 2)
+            if s == 0:
+                xquant(3, 1)
+                xdiag(12, 4)
+            if s == 1:
+                mem_quant2(1)
+            if s >= FL:
+                finish(s - FL)
+            if s + 2 < NT:
+                nmax(s + 2)
+            if s % 2 == 0 and s < 12:
+                xquant(s + 4, 2)
+            if s >= 3 and s % 2 == 1:
+                zcast((s - 3) // 2)
+            if s == NT - 1:
+                zcopy((s - 3) // 2)
+                equant((s - 3) // 2, 0, 2)
+            if s + 2 >= NT:
+                flip(s)
+            if s >= ML:
+                mm2(s - ML)
+        mm2(NT - 3)
+        finish(NT - 4)
+        equant(NT // 2 - 1, 0, 1)
+        zcast(NT // 2 - 1)
+        mm2(NT - 2)
+        evac(NT - 1)
+        zcopy(NT // 2 - 1)
+        equant(NT // 2 - 1, 1, 1)
+        finish(NT - 3)
+        mm2(NT - 1)
+        finish(NT - 2)
+        finish(NT - 1)

@@ -49,8 +49,6 @@ def tile_memorybank2d_pa_kernel(tc, x, memory, out_0, out_1):
         nc.gpsimd.memset(ones_f[:], 1.0)
         nhalf = keep.tile([P, 4], F32)
         nc.gpsimd.memset(nhalf[:], -0.5)
-        nones = keep.tile([P, 2], F32)
-        nc.vector.memset(nones[:], -1.0)
         warm = keep.tile([P, 1], F32)
         nc.vector.memset(warm[:], 1.0)
         warm2 = keep.tile([P, 1], F32)
@@ -242,12 +240,15 @@ def tile_memorybank2d_pa_kernel(tc, x, memory, out_0, out_1):
                                      bias=st[("nm", i)][:], scale=1.0, accum_out=z4[:, i % 2, h:h + 1])
             st[("e", i)] = e
 
-        def zchain(u):
+        def zadd(u):
             z4 = st[("z4", u)]
             zs = small.tile([P, 2], F32, name="zs")
-            nc.gpsimd.tensor_tensor(out=zs[:], in0=z4[:, :, 0], in1=z4[:, :, 1], op=ALU.add)
+            nc.vector.tensor_tensor(out=zs[:], in0=z4[:, :, 0], in1=z4[:, :, 1], op=ALU.add)
+            st[("zs", u)] = zs
+
+        def zrecip(u):
             rz = small.tile([P, 2], F32, name="rz")
-            nc.gpsimd.tensor_tensor(out=rz[:], in0=zs[:], in1=nones[:], op=ALU.pow)
+            nc.vector.reciprocal(out=rz[:], in_=st[("zs", u)][:])
             st[("rz", u)] = rz
 
         def flip(i):
@@ -275,7 +276,10 @@ def tile_memorybank2d_pa_kernel(tc, x, memory, out_0, out_1):
                                   in_=st[("eg", u)][:, w0:w0 + nw].rearrange("p i g n j -> p (i g n j)"))
 
         def zcast(u):
-            zb = ps_tp.tile([P, 2, P], F32, tag="tp", name="zb")
+            if u < NT // 2 - 1:
+                zb = ps_tp.tile([P, 2, P], F32, tag="tp", name="zb")
+            else:
+                zb = ps_sim.tile([P, 2, P], F32, tag="sim", name="zb")
             for w in range(2):
                 nc.tensor.transpose(zb[:, w, :], st[("rz", u)][:, w:w + 1].to_broadcast([P, P]), ident_f[:])
             st[("zb", u)] = zb
@@ -389,8 +393,6 @@ def tile_memorybank2d_pa_kernel(tc, x, memory, out_0, out_1):
         xcopy(4)
         for s in range(NT):
             expo(s)
-            if s % 2 == 1:
-                zchain(s // 2)
             if s >= 1:
                 evac(s - 1)
             if s >= 4 and s % 2 == 0:
@@ -423,12 +425,16 @@ def tile_memorybank2d_pa_kernel(tc, x, memory, out_0, out_1):
                 xdiag(12, 4)
             if s == 1:
                 mem_quant2(1)
+            if s >= 2 and s % 2 == 0:
+                zadd((s - 2) // 2)
             if s >= FL:
                 finish(s - FL)
             if s + 2 < NT:
                 nmax(s + 2)
             if s % 2 == 0 and s < 12:
                 xquant(s + 4, 2)
+            if s >= 2 and s % 2 == 0:
+                zrecip((s - 2) // 2)
             if s >= 3 and s % 2 == 1:
                 zcast((s - 3) // 2)
             if s == NT - 1:
@@ -439,7 +445,9 @@ def tile_memorybank2d_pa_kernel(tc, x, memory, out_0, out_1):
             if s >= ML:
                 mm2(s - ML)
         mm2(NT - 3)
+        zadd(NT // 2 - 1)
         finish(NT - 4)
+        zrecip(NT // 2 - 1)
         equant(NT // 2 - 1, 0, 1)
         zcast(NT // 2 - 1)
         mm2(NT - 2)

@@ -37,7 +37,8 @@ def tile_memorybank2d_pa_kernel(tc, x, memory, out_0, out_1):
         mem_v = memory.rearrange("(g p j) c -> g p j c", g=2, p=P, j=4)
         x_sb = keep.tile([P, B, 4, HW], BF16)
         x_v = x.rearrange("b (p t) h w -> b p t (h w)", t=4)
-        nc.sync.dma_start(out=mem_sb[:, 0], in_=mem_v[0])
+        for j in range(2):
+            nc.sync.dma_start(out=mem_sb[:, 0, j::2], in_=mem_v[0][:, j::2])
         nc.sync.dma_start(out=mem_sb[:, 1], in_=mem_v[1])
         nc.sync.dma_start(out=x_sb[:, 0, :, 0:512], in_=x_v[0][:, :, 0:512])
         nc.sync.dma_start(out=x_sb[:, 0, :, 512:1024], in_=x_v[0][:, :, 512:1024])
@@ -276,7 +277,7 @@ def tile_memorybank2d_pa_kernel(tc, x, memory, out_0, out_1):
                                   in_=st[("eg", u)][:, w0:w0 + nw].rearrange("p i g n j -> p (i g n j)"))
 
         def zcast(u):
-            if u < NT // 2 - 1:
+            if u < NT // 2 - 2:
                 zb = ps_tp.tile([P, 2, P], F32, tag="tp", name="zb")
             else:
                 zb = ps_sim.tile([P, 2, P], F32, tag="sim", name="zb")
@@ -291,7 +292,7 @@ def tile_memorybank2d_pa_kernel(tc, x, memory, out_0, out_1):
         def mm2(i):
             ec, es = st[("ec", i // 2)]
             o = (i % 2) * 2 * P
-            if i < NT - ML - 1:
+            if i < NT - 3:
                 acc = ps_acc.tile([P, 4, P], F32, tag="acc", name="acc")
             else:
                 acc = ps_sim.tile([P, 4, P], F32, tag="sim", name="acc")
@@ -329,6 +330,9 @@ def tile_memorybank2d_pa_kernel(tc, x, memory, out_0, out_1):
         mem_ss_s(0, 0)
         mem_ss_v(0, 1)
         mem_ss_s(0, 1)
+        wt = ps_tp.tile([P, 512], F32, tag="tp", name="wt")
+        for j in range(4):
+            nc.tensor.matmul(wt[:], lhsT=mem_sb[:, 0, j, 0:P], rhs=mem_sb[:, 0, j, :], start=True, stop=True)
         mem_ss_v(1, 0)
         mem_ss_s(1, 0)
         mem_clamp(0)
@@ -353,24 +357,24 @@ def tile_memorybank2d_pa_kernel(tc, x, memory, out_0, out_1):
         xars(0, 2)
         mem_group2(0, 0, "V")
         mem_group2(0, P, "V")
-        mem_group2(0, 2 * P, "V")
         xgram(2, 2, ps_sim, "sim")
         xgram(4, 4, ps_sim, "sim")
         mem_quant1(0)
         xmul(0, 1)
         mem_evac(1, 0, "S")
         xdiag(2, 2)
-        mem_evac(1, 1, "V")
+        mem_evac(1, 1, "S")
+        mem_group2(0, 2 * P, "S")
         mem_group2(0, 3 * P, "S")
-        mem_group2(1, 0, "S")
         xquant(0, 1)
         xspread(2, 2, ps_acc, "acc")
-        xdiag(4, 4)
         mem_quant1(1)
+        xdiag(4, 4)
         xmul(1, 1)
         mm1(0)
         xcols(4, ps_acc, "acc")
         xars(2, 2)
+        mem_group2(1, 0, "S")
         mem_group2(1, P, "S")
         xcols_ars(4)
         warm3 = keep.tile([P, 1], F32)
@@ -440,19 +444,21 @@ def tile_memorybank2d_pa_kernel(tc, x, memory, out_0, out_1):
             if s == NT - 1:
                 zcopy((s - 3) // 2)
                 equant((s - 3) // 2, 0, 2)
+            if s == NT - 2:
+                mm2(s - ML)
             if s + 2 >= NT:
                 flip(s)
-            if s >= ML:
+            if s >= ML and s != NT - 2:
                 mm2(s - ML)
-        mm2(NT - 3)
         zadd(NT // 2 - 1)
-        finish(NT - 4)
-        zrecip(NT // 2 - 1)
-        equant(NT // 2 - 1, 0, 1)
-        zcast(NT // 2 - 1)
-        mm2(NT - 2)
         evac(NT - 1)
+        zrecip(NT // 2 - 1)
+        zcast(NT // 2 - 1)
+        equant(NT // 2 - 1, 0, 1)
+        mm2(NT - 3)
+        finish(NT - 4)
         zcopy(NT // 2 - 1)
+        mm2(NT - 2)
         equant(NT // 2 - 1, 1, 1)
         finish(NT - 3)
         mm2(NT - 1)

@@ -17,8 +17,8 @@ B, C, HW, K = 2, 512, 1024, 1024
 N = B * HW
 NT = N // P
 FLOPS = 2 * N * K * C * 2
-ML = 3
-FL = 4
+ML = 4
+FL = 5
 
 
 def tile_memorybank2d_pa_kernel(tc, x, memory, out_0, out_1):
@@ -114,10 +114,11 @@ def tile_memorybank2d_pa_kernel(tc, x, memory, out_0, out_1):
             nc.scalar.copy(out=rnx[:, i0 * P:(i0 + 4) * P],
                            in_=st[("rnb", i0)][:].rearrange("p a n -> p (a n)"))
 
-        def xmul(i0, n):
+        def xmul(i0, n, eng=None):
+            eng = eng or nc.vector
             fg = work.tile([P, n * P, 4], BF16, name="fg", align_bytes=64)
             b, n0 = i0 // 8, i0 % 8 * P
-            nc.vector.tensor_tensor(
+            eng.tensor_tensor(
                 out=fg[:], in0=x_sb[:, b, :, n0:n0 + n * P].rearrange("p t n -> p n t"),
                 in1=rnx[:, i0 * P:(i0 + n) * P].unsqueeze(2).to_broadcast([P, n * P, 4]), op=ALU.mult)
             st[("fg", i0)] = fg
@@ -225,10 +226,14 @@ def tile_memorybank2d_pa_kernel(tc, x, memory, out_0, out_1):
                                         op=ALU.max, negate=True)
             st[("nm2", i)] = nm2
 
-        def nmax(i):
+        def nmax(i, eng=None):
             nm2 = st[("nm2", i)]
             nm = small.tile([P, 1], F32, name="nm")
-            nc.vector.tensor_tensor(out=nm[:], in0=nm2[:, 0:1], in1=nm2[:, 1:2], op=ALU.min)
+            if eng is nc.gpsimd:
+                nc.gpsimd.tensor_scalar(out=nm[:], in0=nm2[:, 0:1], scalar1=nm2[:, 1:2], scalar2=3.0e38,
+                                        op0=ALU.min, op1=ALU.min)
+            else:
+                nc.vector.tensor_tensor(out=nm[:], in0=nm2[:, 0:1], in1=nm2[:, 1:2], op=ALU.min)
             st[("nm", i)] = nm
 
         def expo(i):
@@ -406,6 +411,7 @@ def tile_memorybank2d_pa_kernel(tc, x, memory, out_0, out_1):
                 xcols(8, ps_acc, "acc")
             if s + 2 < NT:
                 mm1(s + 2)
+            if s + 2 < NT or s == NT - 1:
                 flip(s)
             if s == 1:
                 xcols_pow(8)
@@ -418,9 +424,11 @@ def tile_memorybank2d_pa_kernel(tc, x, memory, out_0, out_1):
                 xcast(12, ps_acc, "acc")
             if s == 4:
                 xcopy(12)
-            if s >= 3 and s % 2 == 1 and s + 2 < NT:
-                equant((s - 3) // 2, 0, 2)
-            if s % 2 == 0 and s < 12:
+            if s >= ML:
+                mm2(s - ML)
+            if s == NT - 2:
+                flip(s)
+            if s % 2 == 0 and s < 6:
                 xmul(s + 4, 2)
             if s + 2 < NT:
                 rowmax(s + 2)
@@ -429,31 +437,33 @@ def tile_memorybank2d_pa_kernel(tc, x, memory, out_0, out_1):
                 xdiag(12, 4)
             if s == 1:
                 mem_quant2(1)
+            if s == 4:
+                xquant(s + 4, 2)
+            if s % 2 == 1 and s < 4:
+                xquant(s + 3, 2)
             if s >= 2 and s % 2 == 0:
                 zadd((s - 2) // 2)
             if s >= FL:
                 finish(s - FL)
             if s + 2 < NT:
-                nmax(s + 2)
-            if s % 2 == 0 and s < 12:
-                xquant(s + 4, 2)
+                nmax(s + 2, nc.gpsimd if s % 2 == 0 else nc.vector)
+            if s % 2 == 0 and 4 <= s < 10:
+                xmul(s + 6, 2, nc.gpsimd)
             if s >= 2 and s % 2 == 0:
                 zrecip((s - 2) // 2)
             if s >= 3 and s % 2 == 1:
-                zcast((s - 3) // 2)
-            if s == NT - 1:
-                zcopy((s - 3) // 2)
                 equant((s - 3) // 2, 0, 2)
-            if s == NT - 2:
-                mm2(s - ML)
-            if s + 2 >= NT:
-                flip(s)
-            if s >= ML and s != NT - 2:
-                mm2(s - ML)
+            if s % 2 == 1 and 4 <= s < 10:
+                xquant(s + 5, 2)
+            if s >= 3 and s % 2 == 1:
+                zcast((s - 3) // 2)
         zadd(NT // 2 - 1)
+        zcopy(NT // 2 - 2)
         evac(NT - 1)
         zrecip(NT // 2 - 1)
         zcast(NT // 2 - 1)
+        mm2(NT - 4)
+        finish(NT - 5)
         equant(NT // 2 - 1, 0, 1)
         mm2(NT - 3)
         finish(NT - 4)

@@ -116,7 +116,10 @@ def tile_memorybank2d_pa_kernel(tc, x, memory, out_0, out_1):
 
         def xmul(i0, n, eng=None):
             eng = eng or nc.vector
-            fg = work.tile([P, n * P, 4], BF16, name="fg", align_bytes=64)
+            if i0 < 8:
+                fg = work.tile([P, n * P, 4], BF16, name="fg", align_bytes=64)
+            else:
+                fg = keep.tile([P, n * P, 4], BF16, name="fgl", align_bytes=64)
             b, n0 = i0 // 8, i0 % 8 * P
             eng.tensor_tensor(
                 out=fg[:], in0=x_sb[:, b, :, n0:n0 + n * P].rearrange("p t n -> p n t"),
@@ -233,7 +236,7 @@ def tile_memorybank2d_pa_kernel(tc, x, memory, out_0, out_1):
                 nc.gpsimd.tensor_scalar(out=nm[:], in0=nm2[:, 0:1], scalar1=nm2[:, 1:2], scalar2=3.0e38,
                                         op0=ALU.min, op1=ALU.min)
             else:
-                nc.vector.tensor_tensor(out=nm[:], in0=nm2[:, 0:1], in1=nm2[:, 1:2], op=ALU.min)
+                nc.vector.tensor_reduce(out=nm[:], in_=nm2[:], axis=AX.X, op=ALU.min)
             st[("nm", i)] = nm
 
         def expo(i):
@@ -249,7 +252,7 @@ def tile_memorybank2d_pa_kernel(tc, x, memory, out_0, out_1):
         def zadd(u):
             z4 = st[("z4", u)]
             zs = small.tile([P, 2], F32, name="zs")
-            nc.vector.tensor_tensor(out=zs[:], in0=z4[:, :, 0], in1=z4[:, :, 1], op=ALU.add)
+            nc.vector.tensor_reduce(out=zs[:], in_=z4[:], axis=AX.X, op=ALU.add)
             st[("zs", u)] = zs
 
         def zrecip(u):
@@ -384,7 +387,6 @@ def tile_memorybank2d_pa_kernel(tc, x, memory, out_0, out_1):
         xcols_ars(4)
         warm3 = keep.tile([P, 1], F32)
         nc.scalar.activation(out=warm3[:], in_=st[("rq", 4)][:, 0:1], func=ACT.Exp)
-        mem_group2(1, 2 * P, "S")
         xgram(8, 4, ps_tp, "tp")
         rowmax(0)
         xquant(1, 1)
@@ -399,7 +401,6 @@ def tile_memorybank2d_pa_kernel(tc, x, memory, out_0, out_1):
         nmax(1)
         xmul(3, 1)
         xdiag(8, 4)
-        xcopy(4)
         for s in range(NT):
             expo(s)
             if s >= 1:
@@ -407,11 +408,14 @@ def tile_memorybank2d_pa_kernel(tc, x, memory, out_0, out_1):
             if s >= 4 and s % 2 == 0:
                 zcopy((s - 4) // 2)
             if s == 0:
-                mem_group2(1, 3 * P, "S")
+                xcopy(4)
+                mem_group2(1, 2 * P, "S")
                 xcols(8, ps_acc, "acc")
+            if s == 1:
+                mem_group2(1, 3 * P, "S")
             if s + 2 < NT:
                 mm1(s + 2)
-            if s + 2 < NT or s == NT - 1:
+            if s < NT - 1:
                 flip(s)
             if s == 1:
                 xcols_pow(8)
@@ -426,7 +430,7 @@ def tile_memorybank2d_pa_kernel(tc, x, memory, out_0, out_1):
                 xcopy(12)
             if s >= ML:
                 mm2(s - ML)
-            if s == NT - 2:
+            if s == NT - 1:
                 flip(s)
             if s % 2 == 0 and s < 6:
                 xmul(s + 4, 2)
@@ -443,15 +447,19 @@ def tile_memorybank2d_pa_kernel(tc, x, memory, out_0, out_1):
                 xquant(s + 3, 2)
             if s >= 2 and s % 2 == 0:
                 zadd((s - 2) // 2)
+            if s == NT - 1:
+                equant((s - 3) // 2, 0, 2)
             if s >= FL:
                 finish(s - FL)
             if s + 2 < NT:
-                nmax(s + 2, nc.gpsimd if s % 2 == 0 else nc.vector)
+                nmax(s + 2)
             if s % 2 == 0 and 4 <= s < 10:
                 xmul(s + 6, 2, nc.gpsimd)
-            if s >= 2 and s % 2 == 0:
+            if s % 2 == 0 and s >= FL:
                 zrecip((s - 2) // 2)
-            if s >= 3 and s % 2 == 1:
+            if s % 2 == 1 and 3 <= s <= FL:
+                zrecip((s - 3) // 2)
+            if s >= 3 and s % 2 == 1 and s < NT - 1:
                 equant((s - 3) // 2, 0, 2)
             if s % 2 == 1 and 4 <= s < 10:
                 xquant(s + 5, 2)
@@ -460,17 +468,17 @@ def tile_memorybank2d_pa_kernel(tc, x, memory, out_0, out_1):
         zadd(NT // 2 - 1)
         zcopy(NT // 2 - 2)
         evac(NT - 1)
-        zrecip(NT // 2 - 1)
-        zcast(NT // 2 - 1)
-        mm2(NT - 4)
-        finish(NT - 5)
         equant(NT // 2 - 1, 0, 1)
+        finish(NT - 5)
+        zrecip(NT // 2 - 1)
+        mm2(NT - 4)
+        zcast(NT // 2 - 1)
         mm2(NT - 3)
-        finish(NT - 4)
         zcopy(NT // 2 - 1)
         mm2(NT - 2)
         equant(NT // 2 - 1, 1, 1)
-        finish(NT - 3)
+        finish(NT - 4)
         mm2(NT - 1)
+        finish(NT - 3)
         finish(NT - 2)
         finish(NT - 1)

@@ -17,8 +17,8 @@ B, C, HW, K = 2, 512, 1024, 1024
 N = B * HW
 NT = N // P
 FLOPS = 2 * N * K * C * 2
-ML = 4
-FL = 5
+ML = 3
+FL = 4
 
 
 def tile_memorybank2d_pa_kernel(tc, x, memory, out_0, out_1):
@@ -116,7 +116,7 @@ def tile_memorybank2d_pa_kernel(tc, x, memory, out_0, out_1):
 
         def xmul(i0, n, eng=None):
             eng = eng or nc.vector
-            if i0 < 8:
+            if i0 < 4:
                 fg = work.tile([P, n * P, 4], BF16, name="fg", align_bytes=64)
             else:
                 fg = keep.tile([P, n * P, 4], BF16, name="fgl", align_bytes=64)
@@ -399,86 +399,78 @@ def tile_memorybank2d_pa_kernel(tc, x, memory, out_0, out_1):
         rowmax(1)
         xquant(2, 1)
         nmax(1)
-        xmul(3, 1)
         xdiag(8, 4)
+        xmul(3, 1)
         for s in range(NT):
+            even = s % 2 == 0
             expo(s)
-            if s >= 1:
-                evac(s - 1)
-            if s >= 4 and s % 2 == 0:
-                zcopy((s - 4) // 2)
-            if s == 0:
-                xcopy(4)
-                mem_group2(1, 2 * P, "S")
-                xcols(8, ps_acc, "acc")
-            if s == 1:
-                mem_group2(1, 3 * P, "S")
-            if s + 2 < NT:
-                mm1(s + 2)
-            if s < NT - 1:
-                flip(s)
             if s == 1:
                 xcols_pow(8)
-                xcols(12, ps_acc, "acc")
-            if s == 2:
-                xcols_pow(12)
-                xcast(8, ps_acc, "acc")
+            if s >= 1:
+                evac(s - 1)
+            if s >= 3 and not even:
+                zcopy((s - 3) // 2)
+            if s == 0:
+                xcopy(4)
+            if s == 1:
+                mem_group2(1, 2 * P, "S")
+                mem_group2(1, 3 * P, "S")
             if s == 3:
                 xcopy(8)
-                xcast(12, ps_acc, "acc")
-            if s == 4:
+            if s == 6:
                 xcopy(12)
-            if s >= ML:
-                mm2(s - ML)
-            if s == NT - 1:
-                flip(s)
-            if s % 2 == 0 and s < 6:
-                xmul(s + 4, 2)
+            if s + 2 < NT:
+                mm1(s + 2)
+            if s == 1:
+                xdiag(12, 4)
+            flip(s)
+            if s == 0:
+                xcols(8, ps_acc, "acc")
+                xmul(4, 2)
+            if s == 1:
+                xmul(6, 2, nc.gpsimd)
+            if s == 2:
+                xcast(8, ps_acc, "acc")
+                xcols(12, ps_acc, "acc")
+            if s == 5:
+                xcast(12, ps_tp, "tp")
+            if even and s >= 2:
+                zrecip((s - 2) // 2)
+                zcast((s - 2) // 2)
             if s + 2 < NT:
                 rowmax(s + 2)
             if s == 0:
                 xquant(3, 1)
-                xdiag(12, 4)
-            if s == 1:
+            if s == 2:
                 mem_quant2(1)
-            if s == 4:
-                xquant(s + 4, 2)
-            if s % 2 == 1 and s < 4:
-                xquant(s + 3, 2)
-            if s >= 2 and s % 2 == 0:
-                zadd((s - 2) // 2)
-            if s == NT - 1:
-                equant((s - 3) // 2, 0, 2)
+            if not even and s < NT - 1:
+                zadd((s - 1) // 2)
             if s >= FL:
                 finish(s - FL)
             if s + 2 < NT:
                 nmax(s + 2)
-            if s % 2 == 0 and 4 <= s < 10:
-                xmul(s + 6, 2, nc.gpsimd)
-            if s % 2 == 0 and s >= FL:
-                zrecip((s - 2) // 2)
-            if s % 2 == 1 and 3 <= s <= FL:
-                zrecip((s - 3) // 2)
-            if s >= 3 and s % 2 == 1 and s < NT - 1:
-                equant((s - 3) // 2, 0, 2)
-            if s % 2 == 1 and 4 <= s < 10:
-                xquant(s + 5, 2)
-            if s >= 3 and s % 2 == 1:
-                zcast((s - 3) // 2)
+            if even and s >= 2:
+                equant((s - 2) // 2, 0, 2)
+            if even and s <= 10:
+                xquant(s + 4, 2)
+                if 4 <= s < 10:
+                    xmul(s + 6, 2, nc.gpsimd)
+            if s == 3:
+                xmul(8, 2, nc.gpsimd)
+                xcols_pow(12)
+            if s >= ML:
+                mm2(s - ML)
+        mm2(NT - 3)
         zadd(NT // 2 - 1)
-        zcopy(NT // 2 - 2)
         evac(NT - 1)
         equant(NT // 2 - 1, 0, 1)
-        finish(NT - 5)
         zrecip(NT // 2 - 1)
-        mm2(NT - 4)
         zcast(NT // 2 - 1)
-        mm2(NT - 3)
         zcopy(NT // 2 - 1)
-        mm2(NT - 2)
-        equant(NT // 2 - 1, 1, 1)
         finish(NT - 4)
-        mm2(NT - 1)
+        equant(NT // 2 - 1, 1, 1)
+        mm2(NT - 2)
         finish(NT - 3)
+        mm2(NT - 1)
         finish(NT - 2)
         finish(NT - 1)

@@ -116,7 +116,7 @@ def tile_memorybank2d_pa_kernel(tc, x, memory, out_0, out_1):
 
         def xmul(i0, n, eng=None):
             eng = eng or nc.vector
-            if i0 < 4:
+            if i0 == 0:
                 fg = work.tile([P, n * P, 4], BF16, name="fg", align_bytes=64)
             else:
                 fg = keep.tile([P, n * P, 4], BF16, name="fgl", align_bytes=64)
@@ -222,12 +222,13 @@ def tile_memorybank2d_pa_kernel(tc, x, memory, out_0, out_1):
                 sims.append(sim)
             st[("sim", i)] = sims
 
-        def rowmax(i):
-            nm2 = small.tile([P, 2], F32, name="nm2")
-            for h in range(2):
+        def rowmax(i, halves=(0, 1)):
+            if 0 in halves:
+                st[("nm2", i)] = small.tile([P, 2], F32, name="nm2")
+            nm2 = st[("nm2", i)]
+            for h in halves:
                 nc.vector.tensor_reduce(out=nm2[:, h:h + 1], in_=st[("sim", i)][h][:], axis=AX.X,
                                         op=ALU.max, negate=True)
-            st[("nm2", i)] = nm2
 
         def nmax(i, eng=None):
             nm2 = st[("nm2", i)]
@@ -315,14 +316,22 @@ def tile_memorybank2d_pa_kernel(tc, x, memory, out_0, out_1):
                         start=(g == 0), stop=(g == 1))
             st[("acc", i)] = acc
 
-        def finish(i):
-            if i % 2 == 0:
+        def finish_g(i, c0):
+            tmp = work.tile([P, 4 - c0, P], F32, name="tmp")
+            nc.scalar.copy(out=tmp[:], in_=st[("acc", i)][:, c0:])
+            st["osb"] = work.tile([P, 4, 2 * P], F32, name="osb")
+            nc.gpsimd.tensor_tensor(
+                out=st["osb"][:, c0:, 0:P], in0=tmp[:],
+                in1=rz_all[:, i * P:(i + 1) * P].unsqueeze(1).to_broadcast([P, 4 - c0, P]), op=ALU.mult)
+
+        def finish(i, c1=4):
+            if i % 2 == 0 and c1 == 4:
                 st["osb"] = work.tile([P, 4, 2 * P], F32, name="osb")
             osb = st["osb"]
             off = (i % 2) * P
             b, n0 = i // 8, (i % 8) * P
-            step = 2 if i == NT - 1 else 4
-            for c0 in range(0, 4, step):
+            step = 2 if i == NT - 1 else c1
+            for c0 in range(0, c1, step):
                 nc.vector.tensor_tensor(
                     out=osb[:, c0:c0 + step, off:off + P], in0=st[("acc", i)][:, c0:c0 + step],
                     in1=rz_all[:, i * P:(i + 1) * P].unsqueeze(1).to_broadcast([P, step, P]), op=ALU.mult)
@@ -353,6 +362,7 @@ def tile_memorybank2d_pa_kernel(tc, x, memory, out_0, out_1):
         mem_flip(0, 0)
         mem_flip(0, 1)
         mem_clamp(1)
+        mem_group2(0, 0, "V")
         xdiag(0, 2)
         mem_ars(1)
         xspread(0, 2, ps_acc, "acc")
@@ -363,7 +373,6 @@ def tile_memorybank2d_pa_kernel(tc, x, memory, out_0, out_1):
         mem_flip(1, 0)
         mem_flip(1, 1)
         xars(0, 2)
-        mem_group2(0, 0, "V")
         mem_group2(0, P, "V")
         xgram(2, 2, ps_sim, "sim")
         xgram(4, 4, ps_sim, "sim")
@@ -383,42 +392,44 @@ def tile_memorybank2d_pa_kernel(tc, x, memory, out_0, out_1):
         xcols(4, ps_acc, "acc")
         xars(2, 2)
         mem_group2(1, 0, "S")
-        mem_group2(1, P, "S")
         xcols_ars(4)
         warm3 = keep.tile([P, 1], F32)
         nc.scalar.activation(out=warm3[:], in_=st[("rq", 4)][:, 0:1], func=ACT.Exp)
-        xgram(8, 4, ps_tp, "tp")
-        rowmax(0)
         xquant(1, 1)
-        nmax(0)
+        xmul(2, 2, nc.gpsimd)
+        rowmax(0)
         mm1(1)
+        xgram(8, 4, ps_tp, "tp")
         xcast(4, ps_acc, "acc")
         xgram(12, 4, ps_tp, "tp")
-        xmul(2, 1)
-        mem_quant2(0)
-        rowmax(1)
-        xquant(2, 1)
-        nmax(1)
+        rowmax(1, (0,))
+        nmax(0)
+        rowmax(1, (1,))
         xdiag(8, 4)
-        xmul(3, 1)
+        nmax(1)
+        xquant(2, 2)
+        mem_group2(1, P, "V")
+        mem_quant2(0)
         for s in range(NT):
             even = s % 2 == 0
             expo(s)
-            if s == 1:
-                xcols_pow(8)
-            if s >= 1:
-                evac(s - 1)
-            if s >= 3 and not even:
-                zcopy((s - 3) // 2)
             if s == 0:
                 xcopy(4)
+                xmul(4, 2, nc.gpsimd)
+            if s >= 1:
+                evac(s - 1)
             if s == 1:
-                mem_group2(1, 2 * P, "S")
-                mem_group2(1, 3 * P, "S")
+                xcols_pow(8)
+            if s >= 3 and not even:
+                zcopy((s - 3) // 2)
+            if s == 1 or s == 2:
+                mem_group2(1, (1 + s) * P, "S")
             if s == 3:
                 xcopy(8)
             if s == 6:
                 xcopy(12)
+            if s - FL in (0, 2, 4, 6, 8, 10):
+                finish_g(s - FL, 3)
             if s + 2 < NT:
                 mm1(s + 2)
             if s == 1:
@@ -426,9 +437,6 @@ def tile_memorybank2d_pa_kernel(tc, x, memory, out_0, out_1):
             flip(s)
             if s == 0:
                 xcols(8, ps_acc, "acc")
-                xmul(4, 2)
-            if s == 1:
-                xmul(6, 2, nc.gpsimd)
             if s == 2:
                 xcast(8, ps_acc, "acc")
                 xcols(12, ps_acc, "acc")
@@ -439,20 +447,23 @@ def tile_memorybank2d_pa_kernel(tc, x, memory, out_0, out_1):
                 zcast((s - 2) // 2)
             if s + 2 < NT:
                 rowmax(s + 2)
-            if s == 0:
-                xquant(3, 1)
-            if s == 2:
-                mem_quant2(1)
+            if s == 1:
+                xquant(4, 2)
+                xmul(6, 2, nc.gpsimd)
             if not even and s < NT - 1:
                 zadd((s - 1) // 2)
-            if s >= FL:
+            if s - FL in (0, 2, 4, 6, 8, 10):
+                finish(s - FL, 3)
+            elif s >= FL:
                 finish(s - FL)
             if s + 2 < NT:
-                nmax(s + 2)
+                nmax(s + 2, nc.gpsimd if s >= 10 else nc.vector)
             if even and s >= 2:
                 equant((s - 2) // 2, 0, 2)
-            if even and s <= 10:
+            if even and 2 <= s <= 10:
                 xquant(s + 4, 2)
+                if s == 2:
+                    mem_quant2(1)
                 if 4 <= s < 10:
                     xmul(s + 6, 2, nc.gpsimd)
             if s == 3:

@@ -114,6 +114,15 @@ def tile_memorybank2d_pa_kernel(tc, x, memory, out_0, out_1):
             nc.scalar.copy(out=rnx[:, i0 * P:(i0 + 4) * P],
                            in_=st[("rnb", i0)][:].rearrange("p a n -> p (a n)"))
 
+        def xmul_shared(i0):
+            fg = keep.tile([P, 2 * P, 4], BF16, name="fgl", align_bytes=64)
+            st[("fg", i0)] = fg
+            for a, eng in ((0, nc.vector), (1, nc.gpsimd)):
+                b, n0 = (i0 + a) // 8, (i0 + a) % 8 * P
+                eng.tensor_tensor(
+                    out=fg[:, a * P:(a + 1) * P], in0=x_sb[:, b, :, n0:n0 + P].rearrange("p t n -> p n t"),
+                    in1=rnx[:, (i0 + a) * P:(i0 + a + 1) * P].unsqueeze(2).to_broadcast([P, P, 4]), op=ALU.mult)
+
         def xmul(i0, n, eng=None):
             eng = eng or nc.vector
             if i0 == 0:
@@ -401,7 +410,6 @@ def tile_memorybank2d_pa_kernel(tc, x, memory, out_0, out_1):
         mm1(1)
         xgram(8, 4, ps_tp, "tp")
         xcast(4, ps_acc, "acc")
-        xgram(12, 4, ps_tp, "tp")
         rowmax(1, (0,))
         nmax(0)
         rowmax(1, (1,))
@@ -428,13 +436,13 @@ def tile_memorybank2d_pa_kernel(tc, x, memory, out_0, out_1):
                 xcopy(8)
             if s == 6:
                 xcopy(12)
-            if s - FL in (0, 2, 4, 6, 8, 10):
+            if s - FL in (4, 6, 8):
                 finish_g(s - FL, 3)
             if s + 2 < NT:
                 mm1(s + 2)
-            if s == 1:
-                xdiag(12, 4)
             flip(s)
+            if s == 1:
+                xgram(12, 4, ps_tp, "tp")
             if s == 0:
                 xcols(8, ps_acc, "acc")
             if s == 2:
@@ -449,17 +457,21 @@ def tile_memorybank2d_pa_kernel(tc, x, memory, out_0, out_1):
                 rowmax(s + 2)
             if s == 1:
                 xquant(4, 2)
-                xmul(6, 2, nc.gpsimd)
             if not even and s < NT - 1:
                 zadd((s - 1) // 2)
-            if s - FL in (0, 2, 4, 6, 8, 10):
+            if s - FL in (4, 6, 8):
                 finish(s - FL, 3)
             elif s >= FL:
                 finish(s - FL)
-            if s + 2 < NT:
+            if s + 2 < NT and s != 2:
                 nmax(s + 2, nc.gpsimd if s >= 10 else nc.vector)
+            if s == 1:
+                xmul_shared(6)
+                xdiag(12, 4)
             if even and s >= 2:
                 equant((s - 2) // 2, 0, 2)
+            if s == 2:
+                nmax(4)
             if even and 2 <= s <= 10:
                 xquant(s + 4, 2)
                 if s == 2:

from contextlib import ExitStack

import concourse.mybir as mybir
from concourse.masks import make_identity

F32 = mybir.dt.float32
BF16 = mybir.dt.bfloat16
U32 = mybir.dt.uint32
U8 = mybir.dt.uint8
FP8X4 = mybir.dt.float8_e4m3fn_x4
ALU = mybir.AluOpType
ACT = mybir.ActivationFunctionType
AX = mybir.AxisListType

P = 128
B, C, HW, K = 2, 512, 1024, 1024
N = B * HW
NT = N // P
FLOPS = 2 * N * K * C * 2
ML = 3
FL = 4


def tile_memorybank2d_pa_kernel(tc, x, memory, out_0, out_1):
    nc = tc.nc
    with ExitStack() as ctx:
        keep = ctx.enter_context(tc.tile_pool(name="keep", bufs=1))
        small = ctx.enter_context(tc.tile_pool(name="small", bufs=8))
        work = ctx.enter_context(tc.tile_pool(name="work", bufs=4))
        ps_sim = ctx.enter_context(tc.psum_pool(name="ps_sim", bufs=4))
        ps_tp = ctx.enter_context(tc.psum_pool(name="ps_tp", bufs=2))
        ps_acc = ctx.enter_context(tc.psum_pool(name="ps_acc", bufs=2))
        ctx.enter_context(tc.manual_schedule())
        st = {}

        mem_sb = keep.tile([P, 2, 4, C], BF16)
        mem_v = memory.rearrange("(g p j) c -> g p j c", g=2, p=P, j=4)
        x_sb = keep.tile([P, B, 4, HW], BF16)
        x_v = x.rearrange("b (p t) h w -> b p t (h w)", t=4)
        for j in range(2):
            nc.sync.dma_start(out=mem_sb[:, 0, j::2], in_=mem_v[0][:, j::2])
        nc.sync.dma_start(out=mem_sb[:, 1], in_=mem_v[1])
        nc.sync.dma_start(out=x_sb[:, 0, :, 0:512], in_=x_v[0][:, :, 0:512])
        nc.sync.dma_start(out=x_sb[:, 0, :, 512:1024], in_=x_v[0][:, :, 512:1024])
        nc.sync.dma_start(out=x_sb[:, 1], in_=x_v[1])

        ident_f = keep.tile([P, P], F32)
        make_identity(nc, ident_f[:])
        ones_f = keep.tile([P, P], F32)
        nc.gpsimd.memset(ones_f[:], 1.0)
        nhalf = keep.tile([P, 4], F32)
        nc.gpsimd.memset(nhalf[:], -0.5)
        warm = keep.tile([P, 1], F32)
        nc.vector.memset(warm[:], 1.0)
        warm2 = keep.tile([P, 1], F32)
        nc.scalar.activation(out=warm2[:], in_=warm[:], func=ACT.Abs_reciprocal_sqrt)

        rnx = keep.tile([P, N], F32)
        fc = keep.tile([P, N], U32, align_bytes=64)
        fs = keep.tile([P, N], U8, align_bytes=64)

        def xgram(i0, n, pool, tag):
            gram = pool.tile([P, n, P], F32, tag=tag, name="gram")
            for a in range(n):
                b, n0 = (i0 + a) // 8, (i0 + a) % 8 * P
                for t in range(4):
                    nc.tensor.matmul(gram[:, a, :], lhsT=x_sb[:, b, t, n0:n0 + P],
                                     rhs=x_sb[:, b, t, n0:n0 + P], start=(t == 0), stop=(t == 3))
            st[("gram", i0)] = gram

        def xdiag(i0, n):
            dm = work.tile([P, n, P], F32, name="dm")
            nc.vector.scalar_tensor_tensor(
                out=dm[:], in0=st[("gram", i0)][:], scalar=1.0e-24,
                in1=ident_f[:].unsqueeze(1).to_broadcast([P, n, P]), op0=ALU.max, op1=ALU.mult)
            st[("dm", i0)] = dm

        def xspread(i0, n, pool, tag):
            ssb = pool.tile([P, n * P], F32, tag=tag, name="ssb")
            nc.tensor.matmul(ssb[:], lhsT=ones_f[:], rhs=st[("dm", i0)][:].rearrange("p a n -> p (a n)"),
                             start=True, stop=True)
            st[("ssb", i0)] = ssb

        def xars(i0, n):
            nc.scalar.activation(out=rnx[:, i0 * P:(i0 + n) * P], in_=st[("ssb", i0)][:],
                                 func=ACT.Abs_reciprocal_sqrt)

        def xcols(i0, pool, tag):
            ssc = pool.tile([P, 4], F32, tag=tag, name="ssc")
            for a in range(4):
                nc.tensor.matmul(ssc[:, a:a + 1], lhsT=st[("dm", i0)][:, a, :], rhs=ones_f[:, 0:1],
                                 start=True, stop=True)
            st[("ssc", i0)] = ssc

        def xcols_ars(i0):
            rq = keep.tile([P, 4], F32, name="rnq%d" % i0)
            nc.scalar.activation(out=rq[:], in_=st[("ssc", i0)][:], func=ACT.Abs_reciprocal_sqrt)
            st[("rq", i0)] = rq

        def xcols_pow(i0):
            sscs = small.tile([P, 4], F32, name="sscs")
            nc.scalar.copy(out=sscs[:], in_=st[("ssc", i0)][:])
            rq = keep.tile([P, 4], F32, name="rnq%d" % i0)
            nc.gpsimd.tensor_tensor(out=rq[:], in0=sscs[:], in1=nhalf[:], op=ALU.pow)
            st[("rq", i0)] = rq

        def xcast(i0, pool, tag):
            rnb = pool.tile([P, 4, P], F32, tag=tag, name="rnb")
            for a in range(4):
                nc.tensor.transpose(rnb[:, a, :], st[("rq", i0)][:, a:a + 1].to_broadcast([P, P]), ident_f[:])
            st[("rnb", i0)] = rnb

        def xcopy(i0):
            nc.scalar.copy(out=rnx[:, i0 * P:(i0 + 4) * P],
                           in_=st[("rnb", i0)][:].rearrange("p a n -> p (a n)"))

        def xmul_shared(i0):
            fg = keep.tile([P, 2 * P, 4], BF16, name="fgl", align_bytes=64)
            st[("fg", i0)] = fg
            for a, eng in ((0, nc.vector), (1, nc.gpsimd)):
                b, n0 = (i0 + a) // 8, (i0 + a) % 8 * P
                eng.tensor_tensor(
                    out=fg[:, a * P:(a + 1) * P], in0=x_sb[:, b, :, n0:n0 + P].rearrange("p t n -> p n t"),
                    in1=rnx[:, (i0 + a) * P:(i0 + a + 1) * P].unsqueeze(2).to_broadcast([P, P, 4]), op=ALU.mult)

        def xmul(i0, n, eng=None):
            eng = eng or nc.vector
            if i0 == 0:
                fg = work.tile([P, n * P, 4], BF16, name="fg", align_bytes=64)
            else:
                fg = keep.tile([P, n * P, 4], BF16, name="fgl", align_bytes=64)
            b, n0 = i0 // 8, i0 % 8 * P
            eng.tensor_tensor(
                out=fg[:], in0=x_sb[:, b, :, n0:n0 + n * P].rearrange("p t n -> p n t"),
                in1=rnx[:, i0 * P:(i0 + n) * P].unsqueeze(2).to_broadcast([P, n * P, 4]), op=ALU.mult)
            st[("fg", i0)] = fg

        def xquant(i0, n):
            cols = slice(i0 * P, (i0 + n) * P)
            nc.vector.quantize_mx(out=fc[:, cols].bitcast(FP8X4), scales=fs[:, cols],
                                  in_=st[("fg", i0)][:].rearrange("p n t -> p (n t)"))

        ss_all = keep.tile([P, 2, 8], F32)
        rn_all = keep.tile([P, 2, 8], F32)
        mn_sb = keep.tile([P, 2, 4, C], BF16)
        g1 = keep.tile([P, 2, 2, P, 2, 4], BF16, align_bytes=64)
        m1c = keep.tile([P, K], U32, align_bytes=64)
        m1s = keep.tile([P, K], U8, align_bytes=64)
        g2 = keep.tile([P, 2, C, 4], BF16, align_bytes=64)
        m2c = keep.tile([P, 2, C], U32, align_bytes=64)
        m2s = keep.tile([P, 2, C], U8, align_bytes=64)

        def mem_ss_v(g, jj):
            junkv = work.tile([P, C], F32, name="junkv")
            nc.vector.scalar_tensor_tensor(
                out=junkv[:], in0=mem_sb[:, g, jj, :], scalar=1.0, in1=mem_sb[:, g, jj, :],
                op0=ALU.mult, op1=ALU.mult, accum_out=ss_all[:, 0, 2 * g + jj:2 * g + jj + 1])

        def mem_ss_s(g, jj):
            junks = work.tile([P, C], F32, name="junks")
            nc.scalar.activation(out=junks[:], in_=mem_sb[:, g, 2 + jj, :], func=ACT.Square,
                                 accum_out=ss_all[:, 1, 2 * g + jj:2 * g + jj + 1])

        def mem_clamp(g):
            cl = small.tile([P, 2, 2], F32, name="cl")
            nc.vector.tensor_scalar(out=cl[:], in0=ss_all[:, :, 2 * g:2 * g + 2], scalar1=1.0e-24,
                                    scalar2=None, op0=ALU.max)
            st[("cl", g)] = cl

        def mem_ars(g):
            nc.scalar.activation(out=rn_all[:, :, 2 * g:2 * g + 2], in_=st[("cl", g)][:],
                                 func=ACT.Abs_reciprocal_sqrt)

        def mem_scale(g, j, eng):
            rcol = rn_all[:, j // 2, 2 * g + j % 2:2 * g + j % 2 + 1]
            if eng == "V":
                nc.vector.tensor_scalar(out=mn_sb[:, g, j, :], in0=mem_sb[:, g, j, :],
                                        scalar1=rcol, scalar2=None, op0=ALU.mult)
            else:
                nc.scalar.activation(out=mn_sb[:, g, j, :], in_=mem_sb[:, g, j, :],
                                     func=ACT.Copy, scale=rcol)

        def mem_flip(g, u):
            tp = ps_tp.tile([P, 2, 2, P], F32, tag="tp", name="tpm")
            for e in range(2):
                words = mn_sb[:, g, 2 * u + e, :].bitcast(F32)
                for w in range(2):
                    nc.tensor.transpose(tp[:, e, w, :], words[:, w::2], ident_f[:])
            st[("tpm", g, u)] = tp

        def mem_evac(g, u, eng):
            src = st[("tpm", g, u)][:].rearrange("p e w q -> p q e w")
            dst = g1[:, g, u].rearrange("p q e t -> p (q e t)").bitcast(F32).rearrange(
                "p (q e w) -> p q e w", e=2, w=2)
            if eng == "V":
                nc.vector.tensor_copy(out=dst, in_=src)
            else:
                nc.scalar.copy(out=dst, in_=src)

        def mem_quant1(g):
            nc.vector.quantize_mx(
                out=m1c[:, g * 512:(g + 1) * 512].bitcast(FP8X4),
                scales=m1s[:, g * 512:(g + 1) * 512],
                in_=g1[:, g].rearrange("p u q e t -> p (u q e t)"))

        def mem_group2(g, c0, eng):
            dst = g2[:, g, c0:c0 + P]
            src = mn_sb[:, g, :, c0:c0 + P].rearrange("p j c -> p c j")
            if eng == "V":
                nc.vector.tensor_copy(out=dst, in_=src)
            else:
                nc.scalar.copy(out=dst, in_=src)

        def mem_quant2(g):
            nc.vector.quantize_mx(out=m2c[:, g, :].bitcast(FP8X4), scales=m2s[:, g, :],
                                  in_=g2[:, g].rearrange("p c j -> p (c j)"))

        rz_all = keep.tile([P, N], F32)
        out_v = out_0.rearrange("b (cc p) h w -> b p cc (h w)", p=P)
        out1_v = out_1.rearrange("b h w -> b (h w)")

        def mm1(i):
            sims = []
            for h in range(2):
                sim = ps_sim.tile([P, 512], F32, tag="sim", name="sim")
                nc.tensor.matmul_mx(
                    out=sim[:],
                    lhsT=fc[:, i * P:(i + 1) * P].bitcast(FP8X4), lhsT_scale=fs[:, i * P:(i + 1) * P],
                    rhs=m1c[:, h * 512:(h + 1) * 512].bitcast(FP8X4),
                    rhs_scale=m1s[:, h * 512:(h + 1) * 512], start=True, stop=True)
                sims.append(sim)
            st[("sim", i)] = sims

        def rowmax(i, halves=(0, 1)):
            if 0 in halves:
                st[("nm2", i)] = small.tile([P, 2], F32, name="nm2")
            nm2 = st[("nm2", i)]
            for h in halves:
                nc.vector.tensor_reduce(out=nm2[:, h:h + 1], in_=st[("sim", i)][h][:], axis=AX.X,
                                        op=ALU.max, negate=True)

        def nmax(i, eng=None):
            nm2 = st[("nm2", i)]
            nm = small.tile([P, 1], F32, name="nm")
            if eng is nc.gpsimd:
                nc.gpsimd.tensor_scalar(out=nm[:], in0=nm2[:, 0:1], scalar1=nm2[:, 1:2], scalar2=3.0e38,
                                        op0=ALU.min, op1=ALU.min)
            else:
                nc.vector.tensor_reduce(out=nm[:], in_=nm2[:], axis=AX.X, op=ALU.min)
            st[("nm", i)] = nm

        def expo(i):
            e = work.tile([P, K], BF16, name="e")
            if i % 2 == 0:
                st[("z4", i // 2)] = small.tile([P, 2, 2], F32, name="z4")
            z4 = st[("z4", i // 2)]
            for h in range(2):
                nc.scalar.activation(out=e[:, h * 512:(h + 1) * 512], in_=st[("sim", i)][h][:], func=ACT.Exp,
                                     bias=st[("nm", i)][:], scale=1.0, accum_out=z4[:, i % 2, h:h + 1])
            st[("e", i)] = e

        def zadd(u):
            z4 = st[("z4", u)]
            zs = small.tile([P, 2], F32, name="zs")
            nc.vector.tensor_reduce(out=zs[:], in_=z4[:], axis=AX.X, op=ALU.add)
            st[("zs", u)] = zs

        def zrecip(u):
            rz = small.tile([P, 2], F32, name="rz")
            nc.vector.reciprocal(out=rz[:], in_=st[("zs", u)][:])
            st[("rz", u)] = rz

        def flip(i):
            words = st[("e", i)][:].bitcast(F32)
            et = ps_tp.tile([P, 4, P], F32, tag="tp", name="et")
            for r in range(4):
                nc.tensor.transpose(et[:, r, :], words[:, r * P:(r + 1) * P], ident_f[:])
            st[("et", i)] = et

        def evac(i):
            if i % 2 == 0:
                st[("eg", i // 2)] = work.tile([P, 2, 2, P, 4], BF16, name="eg", align_bytes=64)
            dst = st[("eg", i // 2)][:, i % 2].rearrange("p g n t -> p (g n t)").bitcast(F32).rearrange(
                "p (g n u) -> p g n u", g=2, u=2)
            nc.scalar.copy(out=dst, in_=st[("et", i)][:].rearrange("p (g u) n -> p g n u", g=2))

        def equant(u, w0, nw):
            if w0 == 0:
                ec = work.tile([P, 4 * P], U32, name="ec", align_bytes=64)
                es = work.tile([P, 4 * P], U8, name="es", align_bytes=64)
                st[("ec", u)] = (ec, es)
            ec, es = st[("ec", u)]
            cols = slice(w0 * 2 * P, (w0 + nw) * 2 * P)
            nc.vector.quantize_mx(out=ec[:, cols].bitcast(FP8X4), scales=es[:, cols],
                                  in_=st[("eg", u)][:, w0:w0 + nw].rearrange("p i g n j -> p (i g n j)"))

        def zcast(u):
            if u < NT // 2 - 2:
                zb = ps_tp.tile([P, 2, P], F32, tag="tp", name="zb")
            else:
                zb = ps_sim.tile([P, 2, P], F32, tag="sim", name="zb")
            for w in range(2):
                nc.tensor.transpose(zb[:, w, :], st[("rz", u)][:, w:w + 1].to_broadcast([P, P]), ident_f[:])
            st[("zb", u)] = zb

        def zcopy(u):
            nc.scalar.copy(out=rz_all[:, 2 * u * P:2 * (u + 1) * P],
                           in_=st[("zb", u)][:].rearrange("p w n -> p (w n)"))

        def mm2(i):
            ec, es = st[("ec", i // 2)]
            o = (i % 2) * 2 * P
            if i < NT - 3:
                acc = ps_acc.tile([P, 4, P], F32, tag="acc", name="acc")
            else:
                acc = ps_sim.tile([P, 4, P], F32, tag="sim", name="acc")
            for cc in range(4):
                for g in range(2):
                    nc.tensor.matmul_mx(
                        out=acc[:, cc, :],
                        lhsT=m2c[:, g, cc * P:(cc + 1) * P].bitcast(FP8X4),
                        lhsT_scale=m2s[:, g, cc * P:(cc + 1) * P],
                        rhs=ec[:, o + g * P:o + (g + 1) * P].bitcast(FP8X4),
                        rhs_scale=es[:, o + g * P:o + (g + 1) * P],
                        start=(g == 0), stop=(g == 1))
            st[("acc", i)] = acc

        def finish_g(i, c0):
            tmp = work.tile([P, 4 - c0, P], F32, name="tmp")
            nc.scalar.copy(out=tmp[:], in_=st[("acc", i)][:, c0:])
            st["osb"] = work.tile([P, 4, 2 * P], F32, name="osb")
            nc.gpsimd.tensor_tensor(
                out=st["osb"][:, c0:, 0:P], in0=tmp[:],
                in1=rz_all[:, i * P:(i + 1) * P].unsqueeze(1).to_broadcast([P, 4 - c0, P]), op=ALU.mult)

        def finish(i, c1=4):
            if i % 2 == 0 and c1 == 4:
                st["osb"] = work.tile([P, 4, 2 * P], F32, name="osb")
            osb = st["osb"]
            off = (i % 2) * P
            b, n0 = i // 8, (i % 8) * P
            step = 2 if i == NT - 1 else c1
            for c0 in range(0, c1, step):
                nc.vector.tensor_tensor(
                    out=osb[:, c0:c0 + step, off:off + P], in0=st[("acc", i)][:, c0:c0 + step],
                    in1=rz_all[:, i * P:(i + 1) * P].unsqueeze(1).to_broadcast([P, step, P]), op=ALU.mult)
                if i >= NT - 2:
                    nc.sync.dma_start(out=out_v[b][:, c0:c0 + step, n0:n0 + P],
                                      in_=osb[:, c0:c0 + step, off:off + P])
            if i % 2 == 1 and i < NT - 2:
                nc.sync.dma_start(out=out_v[b][:, :, n0 - P:n0 + P], in_=osb[:])
            if i % 8 == 7:
                nc.sync.dma_start(out=out1_v[b:b + 1, :], in_=rz_all[0:1, b * HW:(b + 1) * HW])

        mem_ss_v(0, 0)
        mem_ss_s(0, 0)
        mem_ss_v(0, 1)
        mem_ss_s(0, 1)
        wt = ps_tp.tile([P, 512], F32, tag="tp", name="wt")
        for j in range(4):
            nc.tensor.matmul(wt[:], lhsT=mem_sb[:, 0, j, 0:P], rhs=mem_sb[:, 0, j, :], start=True, stop=True)
        mem_ss_v(1, 0)
        mem_ss_s(1, 0)
        mem_clamp(0)
        mem_ars(0)
        mem_ss_v(1, 1)
        mem_ss_s(1, 1)
        xgram(0, 2, ps_acc, "acc")
        for j in range(4):
            mem_scale(0, j, "V")
        mem_flip(0, 0)
        mem_flip(0, 1)
        mem_clamp(1)
        mem_group2(0, 0, "V")
        xdiag(0, 2)
        mem_ars(1)
        xspread(0, 2, ps_acc, "acc")
        for j in range(4):
            mem_scale(1, j, "V")
        mem_evac(0, 0, "S")
        mem_evac(0, 1, "S")
        mem_flip(1, 0)
        mem_flip(1, 1)
        xars(0, 2)
        mem_group2(0, P, "V")
        xgram(2, 2, ps_sim, "sim")
        xgram(4, 4, ps_sim, "sim")
        mem_quant1(0)
        xmul(0, 1)
        mem_evac(1, 0, "S")
        xdiag(2, 2)
        mem_evac(1, 1, "S")
        mem_group2(0, 2 * P, "S")
        mem_group2(0, 3 * P, "S")
        xquant(0, 1)
        xspread(2, 2, ps_acc, "acc")
        mem_quant1(1)
        xdiag(4, 4)
        xmul(1, 1)
        mm1(0)
        xcols(4, ps_acc, "acc")
        xars(2, 2)
        mem_group2(1, 0, "S")
        xcols_ars(4)
        warm3 = keep.tile([P, 1], F32)
        nc.scalar.activation(out=warm3[:], in_=st[("rq", 4)][:, 0:1], func=ACT.Exp)
        xquant(1, 1)
        xmul(2, 2, nc.gpsimd)
        rowmax(0)
        mm1(1)
        xgram(8, 4, ps_tp, "tp")
        xcast(4, ps_acc, "acc")
        rowmax(1, (0,))
        nmax(0)
        rowmax(1, (1,))
        xdiag(8, 4)
        nmax(1)
        xquant(2, 2)
        mem_group2(1, P, "V")
        mem_quant2(0)
        for s in range(NT):
            even = s % 2 == 0
            expo(s)
            if s == 0:
                xcopy(4)
                xmul(4, 2, nc.gpsimd)
            if s >= 1:
                evac(s - 1)
            if s == 1:
                xcols_pow(8)
            if s >= 3 and not even:
                zcopy((s - 3) // 2)
            if s == 1 or s == 2:
                mem_group2(1, (1 + s) * P, "S")
            if s == 3:
                xcopy(8)
            if s == 6:
                xcopy(12)
            if s - FL in (4, 6, 8):
                finish_g(s - FL, 3)
            if s + 2 < NT:
                mm1(s + 2)
            flip(s)
            if s == 1:
                xgram(12, 4, ps_tp, "tp")
            if s == 0:
                xcols(8, ps_acc, "acc")
            if s == 2:
                xcast(8, ps_acc, "acc")
                xcols(12, ps_acc, "acc")
            if s == 5:
                xcast(12, ps_tp, "tp")
            if even and s >= 2:
                zrecip((s - 2) // 2)
                zcast((s - 2) // 2)
            if s + 2 < NT:
                rowmax(s + 2)
            if s == 1:
                xquant(4, 2)
            if not even and s < NT - 1:
                zadd((s - 1) // 2)
            if s - FL in (4, 6, 8):
                finish(s - FL, 3)
            elif s >= FL:
                finish(s - FL)
            if s + 2 < NT and s != 2:
                nmax(s + 2, nc.gpsimd if s >= 10 else nc.vector)
            if s == 1:
                xmul_shared(6)
                xdiag(12, 4)
            if even and s >= 2:
                equant((s - 2) // 2, 0, 2)
            if s == 2:
                nmax(4)
            if even and 2 <= s <= 10:
                xquant(s + 4, 2)
                if s == 2:
                    mem_quant2(1)
                if 4 <= s < 10:
                    xmul(s + 6, 2, nc.gpsimd)
            if s == 3:
                xmul(8, 2, nc.gpsimd)
                xcols_pow(12)
            if s >= ML:
                mm2(s - ML)
        mm2(NT - 3)
        zadd(NT // 2 - 1)
        evac(NT - 1)
        equant(NT // 2 - 1, 0, 1)
        zrecip(NT // 2 - 1)
        zcast(NT // 2 - 1)
        zcopy(NT // 2 - 1)
        finish(NT - 4)
        equant(NT // 2 - 1, 1, 1)
        mm2(NT - 2)
        finish(NT - 3)
        mm2(NT - 1)
        finish(NT - 2)
        finish(NT - 1)
